import numpy as np
import ml_dtypes


def mxq(x, axis, fmt="e4m3"):
    dtype, down = {"e4m3": (ml_dtypes.float8_e4m3fn, 7), "e5m2": (ml_dtypes.float8_e5m2, 14)}[fmt]
    v = np.moveaxis(np.asarray(x, np.float32).astype(ml_dtypes.bfloat16).astype(np.float64), axis, -1)
    blocks = v.reshape(v.shape[:-1] + (-1, 32))
    amax = np.abs(blocks).max(-1, keepdims=True)
    byte = np.maximum(np.where(amax > 0, np.frexp(amax)[1] - 1 + 127, 0) - down, 1)
    scale = np.exp2(byte - 127.0)
    codes = (blocks / scale).astype(np.float32).astype(dtype).astype(np.float64)
    return np.moveaxis((codes * scale).reshape(v.shape), -1, axis)


WIDE = False


def mx_kscale(k):
    if not WIDE:
        return np.ones(k)
    levels = np.array([10, -10, 5, -5, 0])
    a = np.random.permutation(np.resize(levels, k // 512 * 4)).reshape(k // 512, 4)
    idx = np.arange(k)
    return np.exp2(a[idx // 512, idx % 128 // 32])


BF16 = ml_dtypes.bfloat16


def bf(x):
    return np.asarray(x, np.float32).astype(BF16)


def f64(x):
    return np.asarray(x).astype(np.float64)


B, F, P, T = 2, 8192, 128, 2048


def setup_inputs():
    s = np.asarray(mx_kscale(F), np.float64)
    u = np.random.uniform(size=(B, F, P))
    pe = u * 2.0 * T / F
    tm = np.random.uniform(-0.02, 1.02, size=(B, F, 1))
    cf = np.random.uniform(size=(B, F, 1))
    sg = (2.0 * T / F) * (1.0 + 0.1 * np.random.standard_normal(1))
    if np.any(s != 1.0):
        sg = np.array([2.0 ** -5])
        a = np.log2(s / s.min())[None, :, None]
        d = np.where(a > 0, sg[0] * np.sqrt(2.0 * np.log(np.maximum(2.0 ** a - 1.0, 1.0) * 1e10)), 0.0)
        tm = (np.random.randint(0, 4, size=(B, F, 1)) + d) / T
        c = f64(bf(tm)) * T
        gp = np.exp(-0.5 * ((c - np.round(c)) / sg[0]) ** 2)
        pe = u * (64.0 / F) * (gp + 1e-10) / gp
    return {"flashes_pe": bf(pe),
            "flashes_time": bf(tm),
            "flashes_confidence": bf(cf),
            "num_ticks": T,
            "sigma": bf(sg)}


def reference(flashes_pe, flashes_time, flashes_confidence, num_ticks, sigma):
    time_bins = np.clip(f64(flashes_time) * num_ticks, 0.0, num_ticks - 1)[..., 0]
    ticks = np.arange(num_ticks, dtype=np.float64)
    z = (ticks[None, None, :] - time_bins[..., None]) / f64(sigma)
    w = np.exp(-0.5 * z * z)
    w = w / (w.sum(axis=2, keepdims=True) + 1e-10)
    scaled_pe = f64(flashes_pe) * f64(flashes_confidence)
    return mxq(scaled_pe, 1, "e4m3").transpose(0, 2, 1) @ mxq(w, 1, "e4m3")

@@ -1,0 +1,247 @@
+from contextlib import ExitStack
+
+import concourse.mybir as mybir
+
+F32 = mybir.dt.float32
+BF16 = mybir.dt.bfloat16
+I32 = mybir.dt.int32
+U32 = mybir.dt.uint32
+U8 = mybir.dt.uint8
+FP8X4 = mybir.dt.float8_e4m3fn_x4
+ALU = mybir.AluOpType
+ACT = mybir.ActivationFunctionType
+
+P = 128
+PACK = 4
+K_PASS = P * PACK
+EVENTS = 2
+FLASHES = 8192
+CHANNELS = 128
+TICKS = 2048
+GROUPS = FLASHES // K_PASS
+ALL_GROUPS = EVENTS * GROUPS
+N_TILE = 512
+QUANT_COLS = 4096
+HALF = QUANT_COLS // PACK
+HALVES = TICKS // HALF
+BANKS_PER_HALF = HALF // N_TILE
+PE_CHUNK = QUANT_COLS // (PACK * CHANNELS)
+RUN = 4
+VECTOR_PLANE = PACK - 1
+EPS = 1e-10
+
+FLOPS = 2 * EVENTS * FLASHES * CHANNELS * TICKS
+
+
+def planes_view(planes):
+    return planes.rearrange("p j (c i) -> p c j i", i=RUN)
+
+
+def words_view(grouped):
+    return grouped.rearrange("p (c i) j -> p c j i", i=RUN)
+
+
+def tile_flashrecomodel_k_kernel(
+    tc, flashes_pe, flashes_time, flashes_confidence, num_ticks, sigma, out
+):
+    nc = tc.nc
+    assert num_ticks == TICKS
+
+    with ExitStack() as ctx:
+        const = ctx.enter_context(tc.tile_pool(name="const", bufs=1))
+        stage = ctx.enter_context(tc.tile_pool(name="stage", bufs=2))
+        plane_pool = ctx.enter_context(tc.tile_pool(name="plane", bufs=10))
+        small = ctx.enter_context(tc.tile_pool(name="small", bufs=4))
+        w_pool = ctx.enter_context(tc.tile_pool(name="w", bufs=2))
+        mx_pool = ctx.enter_context(tc.tile_pool(name="mx", bufs=3))
+        out_pool = ctx.enter_context(tc.tile_pool(name="result", bufs=4))
+        psum = ctx.enter_context(tc.psum_pool(name="acc", bufs=2))
+
+        time_bf = const.tile([P, ALL_GROUPS, PACK], BF16)
+        nc.sync.dma_start(
+            out=time_bf[:],
+            in_=flashes_time.rearrange("b (g q j) o -> q (b g) (j o)", q=P, j=PACK),
+        )
+        sigma_bf = const.tile([P, 1], BF16)
+        nc.scalar.dma_start(out=sigma_bf[:], in_=sigma.partition_broadcast(P))
+        conf_bf = const.tile([P, ALL_GROUPS, PACK], BF16)
+        nc.scalar.dma_start(
+            out=conf_bf[:],
+            in_=flashes_confidence.rearrange("b (g q j) o -> q (b g) (j o)", q=P, j=PACK),
+        )
+
+        ticks_int = const.tile([P, TICKS], I32)
+        nc.gpsimd.iota(out=ticks_int[:], pattern=[[1, TICKS]], base=0, channel_multiplier=0)
+        ticks = const.tile([P, TICKS], F32)
+        nc.vector.tensor_copy(out=ticks[:], in_=ticks_int[:])
+
+        neg_centre = const.tile([P, ALL_GROUPS * PACK], F32)
+        nc.vector.tensor_scalar(
+            out=neg_centre[:],
+            in0=time_bf[:].rearrange("q g j -> q (g j)"),
+            scalar1=float(TICKS),
+            scalar2=0.0,
+            op0=ALU.mult,
+            op1=ALU.max,
+        )
+        nc.vector.tensor_scalar(
+            out=neg_centre[:],
+            in0=neg_centre[:],
+            scalar1=float(TICKS - 1),
+            scalar2=-1.0,
+            op0=ALU.min,
+            op1=ALU.mult,
+        )
+
+        neg_two_var = const.tile([P, 1], F32)
+        nc.vector.scalar_tensor_tensor(
+            out=neg_two_var[:],
+            in0=sigma_bf[:],
+            scalar=-2.0,
+            in1=sigma_bf[:],
+            op0=ALU.mult,
+            op1=ALU.mult,
+        )
+        exp_scale = const.tile([P, 1], F32)
+        nc.vector.reciprocal(out=exp_scale[:], in_=neg_two_var[:])
+
+        planes = {}
+        sums = {}
+
+        def squares_on_vector(g):
+            col = g * PACK + VECTOR_PLANE
+            plane = plane_pool.tile([P, TICKS], F32)
+            nc.vector.tensor_scalar(
+                out=plane[:],
+                in0=ticks[:],
+                scalar1=neg_centre[:, col : col + 1],
+                scalar2=None,
+                op0=ALU.add,
+            )
+            nc.vector.tensor_tensor(out=plane[:], in0=plane[:], in1=plane[:], op=ALU.mult)
+            planes[(g, VECTOR_PLANE)] = plane
+
+        def gaussians_on_scalar(g):
+            tick_sum = small.tile([P, PACK], F32)
+            sums[g] = tick_sum
+            for j in range(PACK):
+                col = g * PACK + j
+                if j != VECTOR_PLANE:
+                    plane = plane_pool.tile([P, TICKS], F32)
+                    nc.scalar.activation(
+                        out=plane[:],
+                        in_=ticks[:],
+                        func=ACT.Square,
+                        bias=neg_centre[:, col : col + 1],
+                        scale=1.0,
+                    )
+                    planes[(g, j)] = plane
+                squared = planes[(g, j)]
+                nc.scalar.activation(
+                    out=squared[:],
+                    in_=squared[:],
+                    func=ACT.Exp,
+                    scale=exp_scale[:, 0:1],
+                    accum_out=tick_sum[:, j : j + 1],
+                )
+
+        pe_codes = const.tile([P, ALL_GROUPS, CHANNELS], U32, align_bytes=64)
+        pe_scales = const.tile([P, ALL_GROUPS, CHANNELS], U8, align_bytes=64)
+
+        def quantise_pe(chunk):
+            first = chunk * PE_CHUNK
+            b, first_in_event = divmod(first, GROUPS)
+            rows = flashes_pe[b, first_in_event * K_PASS : (first_in_event + PE_CHUNK) * K_PASS, :]
+            pe_raw = stage.tile([P, PE_CHUNK, PACK, CHANNELS], BF16)
+            nc.sync.dma_start(
+                out=pe_raw[:].rearrange("q g j c -> q g (j c)"),
+                in_=rows.rearrange("(g q j) c -> q g (j c)", q=P, j=PACK),
+            )
+            pe_grouped = stage.tile([P, PE_CHUNK, CHANNELS, PACK], BF16, align_bytes=64)
+            for k in range(PE_CHUNK):
+                conf = conf_bf[:, first + k, :].unsqueeze(1).unsqueeze(3)
+                nc.vector.tensor_tensor(
+                    out=words_view(pe_grouped[:, k, :, :]),
+                    in0=planes_view(pe_raw[:, k, :, :]),
+                    in1=conf.to_broadcast([P, CHANNELS // RUN, PACK, RUN]),
+                    op=ALU.mult,
+                )
+            groups = slice(first, first + PE_CHUNK)
+            nc.vector.quantize_mx(
+                out=pe_codes[:, groups, :].rearrange("q g c -> q (g c)").bitcast(FP8X4),
+                scales=pe_scales[:, groups, :].rearrange("q g c -> q (g c)"),
+                in_=pe_grouped[:].rearrange("q g c j -> q (g c j)"),
+            )
+
+        acc = {}
+
+        def finish_group(g):
+            b, g_in_event = divmod(g, GROUPS)
+            inv_sum = small.tile([P, PACK], F32)
+            nc.vector.tensor_scalar(
+                out=inv_sum[:], in0=sums[g][:], scalar1=EPS, scalar2=None, op0=ALU.add
+            )
+            nc.vector.reciprocal(out=inv_sum[:], in_=inv_sum[:])
+
+            w_planes = w_pool.tile([P, PACK, TICKS], BF16)
+            for j in range(PACK):
+                nc.vector.tensor_scalar(
+                    out=w_planes[:, j, :],
+                    in0=planes[(g, j)][:],
+                    scalar1=inv_sum[:, j : j + 1],
+                    scalar2=None,
+                    op0=ALU.mult,
+                )
+
+            grouped_halves = []
+            for h in range(HALVES):
+                w_grouped = w_pool.tile([P, HALF, PACK], BF16, align_bytes=64)
+                nc.vector.tensor_copy(
+                    out=words_view(w_grouped[:]),
+                    in_=planes_view(w_planes[:, :, h * HALF : (h + 1) * HALF]),
+                )
+                grouped_halves.append(w_grouped)
+
+            if g_in_event == 0:
+                for bank in range(HALVES * BANKS_PER_HALF):
+                    acc[bank] = psum.tile([CHANNELS, N_TILE], F32, name="acc%d" % bank)
+
+            for h in range(HALVES):
+                w_codes = mx_pool.tile([P, HALF], U32, align_bytes=64)
+                w_scales = mx_pool.tile([P, HALF], U8, align_bytes=64)
+                nc.vector.quantize_mx(
+                    out=w_codes[:].bitcast(FP8X4),
+                    scales=w_scales[:],
+                    in_=grouped_halves[h][:].rearrange("q t j -> q (t j)"),
+                )
+                for n in range(BANKS_PER_HALF):
+                    cols = slice(n * N_TILE, (n + 1) * N_TILE)
+                    nc.tensor.matmul_mx(
+                        out=acc[h * BANKS_PER_HALF + n][:],
+                        lhsT=pe_codes[:, g, :].bitcast(FP8X4),
+                        lhsT_scale=pe_scales[:, g, :],
+                        rhs=w_codes[:, cols].bitcast(FP8X4),
+                        rhs_scale=w_scales[:, cols],
+                        start=(g_in_event == 0),
+                        stop=(g_in_event == GROUPS - 1),
+                    )
+
+            if g_in_event == GROUPS - 1:
+                for bank in range(HALVES * BANKS_PER_HALF):
+                    result = out_pool.tile([CHANNELS, N_TILE], F32)
+                    nc.scalar.copy(out=result[:], in_=acc[bank][:])
+                    nc.sync.dma_start(
+                        out=out[b, :, bank * N_TILE : (bank + 1) * N_TILE], in_=result[:]
+                    )
+
+        squares_on_vector(0)
+        gaussians_on_scalar(0)
+        squares_on_vector(1)
+        for chunk in range(ALL_GROUPS // PE_CHUNK):
+            quantise_pe(chunk)
+        for g in range(ALL_GROUPS):
+            if g + 1 < ALL_GROUPS:
+                gaussians_on_scalar(g + 1)
+            if g + 2 < ALL_GROUPS:
+                squares_on_vector(g + 2)
+            finish_group(g)

@@ -20,25 +20,34 @@ CHANNELS = 128
 TICKS = 2048
 GROUPS = FLASHES // K_PASS
 ALL_GROUPS = EVENTS * GROUPS
+ALL_PLANES = ALL_GROUPS * PACK
 N_TILE = 512
+BANKS = TICKS // N_TILE
 QUANT_COLS = 4096
 HALF = QUANT_COLS // PACK
 HALVES = TICKS // HALF
 BANKS_PER_HALF = HALF // N_TILE
 PE_CHUNK = QUANT_COLS // (PACK * CHANNELS)
 RUN = 4
-VECTOR_PLANE = PACK - 1
+TICKS_LOW = 128
 EPS = 1e-10
+VECTOR_SHARE = 3
+SHARE_PERIOD = 11
+PLANE_BUFS = 12
 
 FLOPS = 2 * EVENTS * FLASHES * CHANNELS * TICKS
 
 
+def squared_on_vector(plane):
+    return ((plane + 1) * VECTOR_SHARE) % SHARE_PERIOD < VECTOR_SHARE
+
+
 def planes_view(planes):
-    return planes.rearrange("p j (c i) -> p c j i", i=RUN)
+    return planes.rearrange("q j (c i) -> q c j i", i=RUN)
 
 
 def words_view(grouped):
-    return grouped.rearrange("p (c i) j -> p c j i", i=RUN)
+    return grouped.rearrange("q (c i) j -> q c j i", i=RUN)
 
 
 def tile_flashrecomodel_k_kernel(
@@ -49,13 +58,13 @@ def tile_flashrecomodel_k_kernel(
 
     with ExitStack() as ctx:
         const = ctx.enter_context(tc.tile_pool(name="const", bufs=1))
-        stage = ctx.enter_context(tc.tile_pool(name="stage", bufs=2))
-        plane_pool = ctx.enter_context(tc.tile_pool(name="plane", bufs=10))
+        plane_pool = ctx.enter_context(tc.tile_pool(name="plane", bufs=PLANE_BUFS))
         small = ctx.enter_context(tc.tile_pool(name="small", bufs=4))
-        w_pool = ctx.enter_context(tc.tile_pool(name="w", bufs=2))
+        grouped_pool = ctx.enter_context(tc.tile_pool(name="grouped", bufs=2))
         mx_pool = ctx.enter_context(tc.tile_pool(name="mx", bufs=3))
         out_pool = ctx.enter_context(tc.tile_pool(name="result", bufs=4))
-        psum = ctx.enter_context(tc.psum_pool(name="acc", bufs=2))
+        psum = ctx.enter_context(tc.psum_pool(name="acc", bufs=EVENTS))
+        ctx.enter_context(tc.manual_schedule())
 
         time_bf = const.tile([P, ALL_GROUPS, PACK], BF16)
         nc.sync.dma_start(
@@ -69,13 +78,34 @@ def tile_flashrecomodel_k_kernel(
             out=conf_bf[:],
             in_=flashes_confidence.rearrange("b (g q j) o -> q (b g) (j o)", q=P, j=PACK),
         )
+        pe_raw = const.tile([P, ALL_GROUPS, PACK, CHANNELS], BF16)
+        for b in range(EVENTS):
+            nc.sync.dma_start(
+                out=pe_raw[:, b * GROUPS : (b + 1) * GROUPS, :, :].rearrange(
+                    "q g j c -> q g (j c)"
+                ),
+                in_=flashes_pe[b].rearrange("(g q j) c -> q g (j c)", q=P, j=PACK),
+            )
 
-        ticks_int = const.tile([P, TICKS], I32)
-        nc.gpsimd.iota(out=ticks_int[:], pattern=[[1, TICKS]], base=0, channel_multiplier=0)
+        tick_low = const.tile([P, TICKS_LOW], I32)
+        nc.gpsimd.iota(out=tick_low[:], pattern=[[1, TICKS_LOW]], base=0, channel_multiplier=0)
+        tick_high = const.tile([P, TICKS // TICKS_LOW], I32)
+        nc.gpsimd.iota(
+            out=tick_high[:],
+            pattern=[[TICKS_LOW, TICKS // TICKS_LOW]],
+            base=0,
+            channel_multiplier=0,
+        )
         ticks = const.tile([P, TICKS], F32)
-        nc.vector.tensor_copy(out=ticks[:], in_=ticks_int[:])
+        high_low = [P, TICKS // TICKS_LOW, TICKS_LOW]
+        nc.vector.tensor_tensor(
+            out=ticks[:].rearrange("q (h l) -> q h l", l=TICKS_LOW),
+            in0=tick_high[:].unsqueeze(2).to_broadcast(high_low),
+            in1=tick_low[:].unsqueeze(1).to_broadcast(high_low),
+            op=ALU.add,
+        )
 
-        neg_centre = const.tile([P, ALL_GROUPS * PACK], F32)
+        neg_centre = const.tile([P, ALL_PLANES], F32)
         nc.vector.tensor_scalar(
             out=neg_centre[:],
             in0=time_bf[:].rearrange("q g j -> q (g j)"),
@@ -105,41 +135,55 @@ def tile_flashrecomodel_k_kernel(
         exp_scale = const.tile([P, 1], F32)
         nc.vector.reciprocal(out=exp_scale[:], in_=neg_two_var[:])
 
-        planes = {}
-        sums = {}
+        gauss = {}
+        tick_sums = {}
+
+        def vector_planes(g):
+            if g >= ALL_GROUPS:
+                return []
+            return [n for n in range(g * PACK, (g + 1) * PACK) if squared_on_vector(n)]
+
+        def differences_on_vector(g):
+            for n in vector_planes(g):
+                plane = plane_pool.tile([P, TICKS], F32)
+                nc.vector.tensor_scalar(
+                    out=plane[:],
+                    in0=ticks[:],
+                    scalar1=neg_centre[:, n : n + 1],
+                    scalar2=None,
+                    op0=ALU.add,
+                )
+                gauss[n] = plane
 
         def squares_on_vector(g):
-            col = g * PACK + VECTOR_PLANE
-            plane = plane_pool.tile([P, TICKS], F32)
-            nc.vector.tensor_scalar(
-                out=plane[:],
-                in0=ticks[:],
-                scalar1=neg_centre[:, col : col + 1],
-                scalar2=None,
-                op0=ALU.add,
-            )
-            nc.vector.tensor_tensor(out=plane[:], in0=plane[:], in1=plane[:], op=ALU.mult)
-            planes[(g, VECTOR_PLANE)] = plane
+            for n in vector_planes(g):
+                nc.vector.tensor_tensor(
+                    out=gauss[n][:], in0=gauss[n][:], in1=gauss[n][:], op=ALU.mult
+                )
+
+        def square_on_scalar(n):
+            if n < ALL_PLANES and not squared_on_vector(n):
+                plane = plane_pool.tile([P, TICKS], F32)
+                nc.scalar.activation(
+                    out=plane[:],
+                    in_=ticks[:],
+                    func=ACT.Square,
+                    bias=neg_centre[:, n : n + 1],
+                    scale=1.0,
+                )
+                gauss[n] = plane
 
         def gaussians_on_scalar(g):
+            if g >= ALL_GROUPS:
+                return
             tick_sum = small.tile([P, PACK], F32)
-            sums[g] = tick_sum
+            tick_sums[g] = tick_sum
             for j in range(PACK):
-                col = g * PACK + j
-                if j != VECTOR_PLANE:
-                    plane = plane_pool.tile([P, TICKS], F32)
-                    nc.scalar.activation(
-                        out=plane[:],
-                        in_=ticks[:],
-                        func=ACT.Square,
-                        bias=neg_centre[:, col : col + 1],
-                        scale=1.0,
-                    )
-                    planes[(g, j)] = plane
-                squared = planes[(g, j)]
+                n = g * PACK + j
+                square_on_scalar(n + 1)
                 nc.scalar.activation(
-                    out=squared[:],
-                    in_=squared[:],
+                    out=gauss[n][:],
+                    in_=gauss[n][:],
                     func=ACT.Exp,
                     scale=exp_scale[:, 0:1],
                     accum_out=tick_sum[:, j : j + 1],
@@ -149,99 +193,111 @@ def tile_flashrecomodel_k_kernel(
         pe_scales = const.tile([P, ALL_GROUPS, CHANNELS], U8, align_bytes=64)
 
         def quantise_pe(chunk):
-            first = chunk * PE_CHUNK
-            b, first_in_event = divmod(first, GROUPS)
-            rows = flashes_pe[b, first_in_event * K_PASS : (first_in_event + PE_CHUNK) * K_PASS, :]
-            pe_raw = stage.tile([P, PE_CHUNK, PACK, CHANNELS], BF16)
-            nc.sync.dma_start(
-                out=pe_raw[:].rearrange("q g j c -> q g (j c)"),
-                in_=rows.rearrange("(g q j) c -> q g (j c)", q=P, j=PACK),
-            )
-            pe_grouped = stage.tile([P, PE_CHUNK, CHANNELS, PACK], BF16, align_bytes=64)
+            pe_grouped = const.tile([P, PE_CHUNK, CHANNELS, PACK], BF16, align_bytes=64)
             for k in range(PE_CHUNK):
-                conf = conf_bf[:, first + k, :].unsqueeze(1).unsqueeze(3)
+                g = chunk * PE_CHUNK + k
+                conf = conf_bf[:, g, :].unsqueeze(1).unsqueeze(3)
                 nc.vector.tensor_tensor(
                     out=words_view(pe_grouped[:, k, :, :]),
-                    in0=planes_view(pe_raw[:, k, :, :]),
+                    in0=planes_view(pe_raw[:, g, :, :]),
                     in1=conf.to_broadcast([P, CHANNELS // RUN, PACK, RUN]),
                     op=ALU.mult,
                 )
-            groups = slice(first, first + PE_CHUNK)
+            groups = slice(chunk * PE_CHUNK, (chunk + 1) * PE_CHUNK)
             nc.vector.quantize_mx(
                 out=pe_codes[:, groups, :].rearrange("q g c -> q (g c)").bitcast(FP8X4),
                 scales=pe_scales[:, groups, :].rearrange("q g c -> q (g c)"),
                 in_=pe_grouped[:].rearrange("q g c j -> q (g c j)"),
             )
 
+        inv_sums = {}
+        w_planes = {}
+        w_grouped = {}
         acc = {}
 
-        def finish_group(g):
-            b, g_in_event = divmod(g, GROUPS)
+        def add_eps(g):
             inv_sum = small.tile([P, PACK], F32)
             nc.vector.tensor_scalar(
-                out=inv_sum[:], in0=sums[g][:], scalar1=EPS, scalar2=None, op0=ALU.add
+                out=inv_sum[:], in0=tick_sums[g][:], scalar1=EPS, scalar2=None, op0=ALU.add
             )
-            nc.vector.reciprocal(out=inv_sum[:], in_=inv_sum[:])
+            inv_sums[g] = inv_sum
 
-            w_planes = w_pool.tile([P, PACK, TICKS], BF16)
+        def invert_sums(g):
+            nc.vector.reciprocal(out=inv_sums[g][:], in_=inv_sums[g][:])
+
+        def normalise(g):
+            w_plane = const.tile([P, PACK, TICKS], BF16)
             for j in range(PACK):
                 nc.vector.tensor_scalar(
-                    out=w_planes[:, j, :],
-                    in0=planes[(g, j)][:],
-                    scalar1=inv_sum[:, j : j + 1],
+                    out=w_plane[:, j, :],
+                    in0=gauss[g * PACK + j][:],
+                    scalar1=inv_sums[g][:, j : j + 1],
                     scalar2=None,
                     op0=ALU.mult,
                 )
+            w_planes[g] = w_plane
 
-            grouped_halves = []
-            for h in range(HALVES):
-                w_grouped = w_pool.tile([P, HALF, PACK], BF16, align_bytes=64)
-                nc.vector.tensor_copy(
-                    out=words_view(w_grouped[:]),
-                    in_=planes_view(w_planes[:, :, h * HALF : (h + 1) * HALF]),
+        def regroup(g, h):
+            grouped = grouped_pool.tile([P, HALF, PACK], BF16, align_bytes=64)
+            nc.vector.tensor_copy(
+                out=words_view(grouped[:]),
+                in_=planes_view(w_planes[g][:, :, h * HALF : (h + 1) * HALF]),
+            )
+            w_grouped[(g, h)] = grouped
+
+        def quantise_and_multiply(g, h):
+            b, g_in_event = divmod(g, GROUPS)
+            w_codes = mx_pool.tile([P, HALF], U32, align_bytes=64)
+            w_scales = mx_pool.tile([P, HALF], U8, align_bytes=64)
+            nc.vector.quantize_mx(
+                out=w_codes[:].bitcast(FP8X4),
+                scales=w_scales[:],
+                in_=w_grouped[(g, h)][:].rearrange("q t j -> q (t j)"),
+            )
+            for n in range(BANKS_PER_HALF):
+                bank = h * BANKS_PER_HALF + n
+                if g_in_event == 0:
+                    acc[(b, bank)] = psum.tile([CHANNELS, N_TILE], F32, name="acc%d" % bank)
+                cols = slice(n * N_TILE, (n + 1) * N_TILE)
+                nc.tensor.matmul_mx(
+                    out=acc[(b, bank)][:],
+                    lhsT=pe_codes[:, g, :].bitcast(FP8X4),
+                    lhsT_scale=pe_scales[:, g, :],
+                    rhs=w_codes[:, cols].bitcast(FP8X4),
+                    rhs_scale=w_scales[:, cols],
+                    start=(g_in_event == 0),
+                    stop=(g_in_event == GROUPS - 1),
                 )
-                grouped_halves.append(w_grouped)
 
-            if g_in_event == 0:
-                for bank in range(HALVES * BANKS_PER_HALF):
-                    acc[bank] = psum.tile([CHANNELS, N_TILE], F32, name="acc%d" % bank)
-
-            for h in range(HALVES):
-                w_codes = mx_pool.tile([P, HALF], U32, align_bytes=64)
-                w_scales = mx_pool.tile([P, HALF], U8, align_bytes=64)
-                nc.vector.quantize_mx(
-                    out=w_codes[:].bitcast(FP8X4),
-                    scales=w_scales[:],
-                    in_=grouped_halves[h][:].rearrange("q t j -> q (t j)"),
+        def store_event(b):
+            for bank in range(BANKS):
+                result = out_pool.tile([CHANNELS, N_TILE], F32)
+                nc.scalar.copy(out=result[:], in_=acc[(b, bank)][:])
+                nc.sync.dma_start(
+                    out=out[b, :, bank * N_TILE : (bank + 1) * N_TILE], in_=result[:]
                 )
-                for n in range(BANKS_PER_HALF):
-                    cols = slice(n * N_TILE, (n + 1) * N_TILE)
-                    nc.tensor.matmul_mx(
-                        out=acc[h * BANKS_PER_HALF + n][:],
-                        lhsT=pe_codes[:, g, :].bitcast(FP8X4),
-                        lhsT_scale=pe_scales[:, g, :],
-                        rhs=w_codes[:, cols].bitcast(FP8X4),
-                        rhs_scale=w_scales[:, cols],
-                        start=(g_in_event == 0),
-                        stop=(g_in_event == GROUPS - 1),
-                    )
 
-            if g_in_event == GROUPS - 1:
-                for bank in range(HALVES * BANKS_PER_HALF):
-                    result = out_pool.tile([CHANNELS, N_TILE], F32)
-                    nc.scalar.copy(out=result[:], in_=acc[bank][:])
-                    nc.sync.dma_start(
-                        out=out[b, :, bank * N_TILE : (bank + 1) * N_TILE], in_=result[:]
-                    )
-
-        squares_on_vector(0)
+        square_on_scalar(0)
+        for g in range(2):
+            differences_on_vector(g)
+            squares_on_vector(g)
         gaussians_on_scalar(0)
-        squares_on_vector(1)
-        for chunk in range(ALL_GROUPS // PE_CHUNK):
-            quantise_pe(chunk)
+        quantise_pe(0)
         for g in range(ALL_GROUPS):
-            if g + 1 < ALL_GROUPS:
-                gaussians_on_scalar(g + 1)
-            if g + 2 < ALL_GROUPS:
-                squares_on_vector(g + 2)
-            finish_group(g)
+            gaussians_on_scalar(g + 1)
+            if g == ALL_GROUPS - 1:
+                store_event(0)
+            if g % PE_CHUNK == 0 and g + PE_CHUNK < ALL_GROUPS:
+                quantise_pe(g // PE_CHUNK + 1)
+            add_eps(g)
+            if g > 0:
+                quantise_and_multiply(g - 1, 1)
+            invert_sums(g)
+            differences_on_vector(g + 2)
+            normalise(g)
+            squares_on_vector(g + 2)
+            regroup(g, 0)
+            regroup(g, 1)
+            quantise_and_multiply(g, 0)
+        quantise_and_multiply(ALL_GROUPS - 1, 1)
+        store_event(EVENTS - 1)

@@ -1,6 +1,7 @@
 from contextlib import ExitStack
 
 import concourse.mybir as mybir
+from concourse.masks import make_identity
 
 F32 = mybir.dt.float32
 BF16 = mybir.dt.bfloat16
@@ -33,7 +34,7 @@ TICKS_LOW = 128
 EPS = 1e-10
 VECTOR_SHARE = 3
 SHARE_PERIOD = 11
-PLANE_BUFS = 12
+GROUP_BUFS = 4
 
 FLOPS = 2 * EVENTS * FLASHES * CHANNELS * TICKS
 
@@ -58,12 +59,14 @@ def tile_flashrecomodel_k_kernel(
 
     with ExitStack() as ctx:
         const = ctx.enter_context(tc.tile_pool(name="const", bufs=1))
-        plane_pool = ctx.enter_context(tc.tile_pool(name="plane", bufs=PLANE_BUFS))
+        gauss_pool = ctx.enter_context(tc.tile_pool(name="gauss", bufs=GROUP_BUFS))
         small = ctx.enter_context(tc.tile_pool(name="small", bufs=4))
         grouped_pool = ctx.enter_context(tc.tile_pool(name="grouped", bufs=2))
-        mx_pool = ctx.enter_context(tc.tile_pool(name="mx", bufs=3))
+        mx_pool = ctx.enter_context(tc.tile_pool(name="mx", bufs=4))
+        pe_pool = ctx.enter_context(tc.tile_pool(name="pe", bufs=2))
         out_pool = ctx.enter_context(tc.tile_pool(name="result", bufs=4))
-        psum = ctx.enter_context(tc.psum_pool(name="acc", bufs=EVENTS))
+        psum = ctx.enter_context(tc.psum_pool(name="acc", bufs=1))
+        inv_psum = ctx.enter_context(tc.psum_pool(name="inv", bufs=2))
         ctx.enter_context(tc.manual_schedule())
 
         time_bf = const.tile([P, ALL_GROUPS, PACK], BF16)
@@ -78,14 +81,24 @@ def tile_flashrecomodel_k_kernel(
             out=conf_bf[:],
             in_=flashes_confidence.rearrange("b (g q j) o -> q (b g) (j o)", q=P, j=PACK),
         )
-        pe_raw = const.tile([P, ALL_GROUPS, PACK, CHANNELS], BF16)
-        for b in range(EVENTS):
+        pe_raw = {}
+
+        def load_pe(chunk):
+            b, first = divmod(chunk * PE_CHUNK, GROUPS)
+            raw = pe_pool.tile([P, PE_CHUNK, PACK, CHANNELS], BF16)
             nc.sync.dma_start(
-                out=pe_raw[:, b * GROUPS : (b + 1) * GROUPS, :, :].rearrange(
-                    "q g j c -> q g (j c)"
-                ),
-                in_=flashes_pe[b].rearrange("(g q j) c -> q g (j c)", q=P, j=PACK),
+                out=raw[:].rearrange("q g j c -> q g (j c)"),
+                in_=flashes_pe[b].rearrange("(g q j) c -> q g (j c)", q=P, j=PACK)[
+                    :, first : first + PE_CHUNK, :
+                ],
             )
+            pe_raw[chunk] = raw
+
+        load_pe(0)
+        load_pe(1)
+
+        identity = const.tile([P, P], F32)
+        make_identity(nc, identity[:])
 
         tick_low = const.tile([P, TICKS_LOW], I32)
         nc.gpsimd.iota(out=tick_low[:], pattern=[[1, TICKS_LOW]], base=0, channel_multiplier=0)
@@ -138,6 +151,13 @@ def tile_flashrecomodel_k_kernel(
         gauss = {}
         tick_sums = {}
 
+        def plane_of(n):
+            g, j = divmod(n, PACK)
+            if g not in gauss:
+                group_tile = gauss_pool.tile([P, PACK, TICKS], F32)
+                gauss[g] = group_tile
+            return gauss[g][:, j, :]
+
         def vector_planes(g):
             if g >= ALL_GROUPS:
                 return []
@@ -145,49 +165,45 @@ def tile_flashrecomodel_k_kernel(
 
         def differences_on_vector(g):
             for n in vector_planes(g):
-                plane = plane_pool.tile([P, TICKS], F32)
                 nc.vector.tensor_scalar(
-                    out=plane[:],
+                    out=plane_of(n),
                     in0=ticks[:],
                     scalar1=neg_centre[:, n : n + 1],
                     scalar2=None,
                     op0=ALU.add,
                 )
-                gauss[n] = plane
 
         def squares_on_vector(g):
             for n in vector_planes(g):
-                nc.vector.tensor_tensor(
-                    out=gauss[n][:], in0=gauss[n][:], in1=gauss[n][:], op=ALU.mult
-                )
+                plane = plane_of(n)
+                nc.vector.tensor_tensor(out=plane, in0=plane, in1=plane, op=ALU.mult)
 
         def square_on_scalar(n):
             if n < ALL_PLANES and not squared_on_vector(n):
-                plane = plane_pool.tile([P, TICKS], F32)
                 nc.scalar.activation(
-                    out=plane[:],
+                    out=plane_of(n),
                     in_=ticks[:],
                     func=ACT.Square,
                     bias=neg_centre[:, n : n + 1],
                     scale=1.0,
                 )
-                gauss[n] = plane
 
-        def gaussians_on_scalar(g):
-            if g >= ALL_GROUPS:
+        def gaussian_on_scalar(n):
+            if n >= ALL_PLANES:
                 return
-            tick_sum = small.tile([P, PACK], F32)
-            tick_sums[g] = tick_sum
-            for j in range(PACK):
-                n = g * PACK + j
-                square_on_scalar(n + 1)
-                nc.scalar.activation(
-                    out=gauss[n][:],
-                    in_=gauss[n][:],
-                    func=ACT.Exp,
-                    scale=exp_scale[:, 0:1],
-                    accum_out=tick_sum[:, j : j + 1],
-                )
+            g, j = divmod(n, PACK)
+            if j == 0:
+                tick_sum = small.tile([P, PACK], F32)
+                tick_sums[g] = tick_sum
+            square_on_scalar(n + 1)
+            plane = plane_of(n)
+            nc.scalar.activation(
+                out=plane,
+                in_=plane,
+                func=ACT.Exp,
+                scale=exp_scale[:, 0:1],
+                accum_out=tick_sums[g][:, j : j + 1],
+            )
 
         pe_codes = const.tile([P, ALL_GROUPS, CHANNELS], U32, align_bytes=64)
         pe_scales = const.tile([P, ALL_GROUPS, CHANNELS], U8, align_bytes=64)
@@ -199,10 +215,12 @@ def tile_flashrecomodel_k_kernel(
                 conf = conf_bf[:, g, :].unsqueeze(1).unsqueeze(3)
                 nc.vector.tensor_tensor(
                     out=words_view(pe_grouped[:, k, :, :]),
-                    in0=planes_view(pe_raw[:, g, :, :]),
+                    in0=planes_view(pe_raw[chunk][:, k, :, :]),
                     in1=conf.to_broadcast([P, CHANNELS // RUN, PACK, RUN]),
                     op=ALU.mult,
                 )
+            if chunk + 2 < ALL_GROUPS // PE_CHUNK:
+                load_pe(chunk + 2)
             groups = slice(chunk * PE_CHUNK, (chunk + 1) * PE_CHUNK)
             nc.vector.quantize_mx(
                 out=pe_codes[:, groups, :].rearrange("q g c -> q (g c)").bitcast(FP8X4),
@@ -211,7 +229,7 @@ def tile_flashrecomodel_k_kernel(
             )
 
         inv_sums = {}
-        w_planes = {}
+        inv_factors = {}
         w_grouped = {}
         acc = {}
 
@@ -225,23 +243,21 @@ def tile_flashrecomodel_k_kernel(
         def invert_sums(g):
             nc.vector.reciprocal(out=inv_sums[g][:], in_=inv_sums[g][:])
 
-        def normalise(g):
-            w_plane = const.tile([P, PACK, TICKS], BF16)
-            for j in range(PACK):
-                nc.vector.tensor_scalar(
-                    out=w_plane[:, j, :],
-                    in0=gauss[g * PACK + j][:],
-                    scalar1=inv_sums[g][:, j : j + 1],
-                    scalar2=None,
-                    op0=ALU.mult,
-                )
-            w_planes[g] = w_plane
+        def spread_inv(g):
+            bank = inv_psum.tile([P, N_TILE], F32)
+            nc.tensor.matmul(
+                out=bank[:, 0:PACK], lhsT=identity[:], rhs=inv_sums[g][:], start=True, stop=True
+            )
+            inv_factors[g] = bank
 
-        def regroup(g, h):
+        def normalise(g, h):
             grouped = grouped_pool.tile([P, HALF, PACK], BF16, align_bytes=64)
-            nc.vector.tensor_copy(
+            factor = inv_factors[g][:, 0:PACK].unsqueeze(1).unsqueeze(3)
+            nc.vector.tensor_tensor(
                 out=words_view(grouped[:]),
-                in_=planes_view(w_planes[g][:, :, h * HALF : (h + 1) * HALF]),
+                in0=planes_view(gauss[g][:, :, h * HALF : (h + 1) * HALF]),
+                in1=factor.to_broadcast([P, HALF // RUN, PACK, RUN]),
+                op=ALU.mult,
             )
             w_grouped[(g, h)] = grouped
 
@@ -281,23 +297,31 @@ def tile_flashrecomodel_k_kernel(
         for g in range(2):
             differences_on_vector(g)
             squares_on_vector(g)
-        gaussians_on_scalar(0)
+        for j in range(PACK):
+            gaussian_on_scalar(j)
         quantise_pe(0)
+        add_eps(0)
+        differences_on_vector(2)
+        invert_sums(0)
+        spread_inv(0)
+        squares_on_vector(2)
         for g in range(ALL_GROUPS):
-            gaussians_on_scalar(g + 1)
-            if g == ALL_GROUPS - 1:
+            gaussian_on_scalar((g + 1) * PACK)
+            if g == GROUPS:
                 store_event(0)
+            for j in range(1, PACK):
+                gaussian_on_scalar((g + 1) * PACK + j)
+            normalise(g, 0)
             if g % PE_CHUNK == 0 and g + PE_CHUNK < ALL_GROUPS:
                 quantise_pe(g // PE_CHUNK + 1)
-            add_eps(g)
-            if g > 0:
-                quantise_and_multiply(g - 1, 1)
-            invert_sums(g)
-            differences_on_vector(g + 2)
-            normalise(g)
-            squares_on_vector(g + 2)
-            regroup(g, 0)
-            regroup(g, 1)
+            normalise(g, 1)
             quantise_and_multiply(g, 0)
-        quantise_and_multiply(ALL_GROUPS - 1, 1)
+            differences_on_vector(g + 3)
+            if g + 1 < ALL_GROUPS:
+                add_eps(g + 1)
+            quantise_and_multiply(g, 1)
+            squares_on_vector(g + 3)
+            if g + 1 < ALL_GROUPS:
+                invert_sums(g + 1)
+                spread_inv(g + 1)
         store_event(EVENTS - 1)

@@ -24,23 +24,31 @@ ALL_GROUPS = EVENTS * GROUPS
 ALL_PLANES = ALL_GROUPS * PACK
 N_TILE = 512
 BANKS = TICKS // N_TILE
-QUANT_COLS = 4096
-HALF = QUANT_COLS // PACK
-HALVES = TICKS // HALF
+HALVES = 2
+HALF = TICKS // HALVES
 BANKS_PER_HALF = HALF // N_TILE
-PE_CHUNK = QUANT_COLS // (PACK * CHANNELS)
+PE_CHUNK = 8
 RUN = 4
 TICKS_LOW = 128
 EPS = 1e-10
-VECTOR_SHARE = 3
-SHARE_PERIOD = 11
+GPSIMD_END = 512
+VECTOR_END = 1536
 GROUP_BUFS = 4
 
 FLOPS = 2 * EVENTS * FLASHES * CHANNELS * TICKS
 
 
-def squared_on_vector(plane):
-    return ((plane + 1) * VECTOR_SHARE) % SHARE_PERIOD < VECTOR_SHARE
+def squares_of(g):
+    if g == 0:
+        return [], [(1, 0, TICKS), (2, 0, TICKS), (3, 0, TICKS)], [(0, 0, TICKS)]
+    if g == 1:
+        return [], [(1, 0, TICKS)], [(0, 0, TICKS), (2, 0, TICKS), (3, 0, TICKS)]
+    vector_end = VECTOR_END if g < ALL_GROUPS - 2 else GPSIMD_END
+    return (
+        [(0, 0, TICKS), (1, 0, GPSIMD_END)],
+        [(1, GPSIMD_END, vector_end)] if vector_end > GPSIMD_END else [],
+        [(1, vector_end, TICKS), (2, 0, TICKS), (3, 0, TICKS)],
+    )
 
 
 def planes_view(planes):
@@ -60,27 +68,28 @@ def tile_flashrecomodel_k_kernel(
     with ExitStack() as ctx:
         const = ctx.enter_context(tc.tile_pool(name="const", bufs=1))
         gauss_pool = ctx.enter_context(tc.tile_pool(name="gauss", bufs=GROUP_BUFS))
-        small = ctx.enter_context(tc.tile_pool(name="small", bufs=4))
-        grouped_pool = ctx.enter_context(tc.tile_pool(name="grouped", bufs=2))
+        small = ctx.enter_context(tc.tile_pool(name="small", bufs=6))
+        grouped_pool = ctx.enter_context(tc.tile_pool(name="grouped", bufs=3))
         mx_pool = ctx.enter_context(tc.tile_pool(name="mx", bufs=4))
         pe_pool = ctx.enter_context(tc.tile_pool(name="pe", bufs=2))
+        pe_mx_pool = ctx.enter_context(tc.tile_pool(name="pe_mx", bufs=4))
         out_pool = ctx.enter_context(tc.tile_pool(name="result", bufs=4))
         psum = ctx.enter_context(tc.psum_pool(name="acc", bufs=1))
-        inv_psum = ctx.enter_context(tc.psum_pool(name="inv", bufs=2))
+        factor_psum = ctx.enter_context(tc.psum_pool(name="factor", bufs=2))
         ctx.enter_context(tc.manual_schedule())
 
-        time_bf = const.tile([P, ALL_GROUPS, PACK], BF16)
+        flash_rows = const.tile([P, K_PASS], BF16)
+        nc.vector.memset(flash_rows[:], 0.0)
         nc.sync.dma_start(
-            out=time_bf[:],
-            in_=flashes_time.rearrange("b (g q j) o -> q (b g) (j o)", q=P, j=PACK),
+            out=flash_rows[0:ALL_GROUPS, :],
+            in_=flashes_time.rearrange("b (g k) o -> (b g) (k o)", k=K_PASS),
+        )
+        nc.scalar.dma_start(
+            out=flash_rows[ALL_GROUPS : 2 * ALL_GROUPS, :],
+            in_=flashes_confidence.rearrange("b (g k) o -> (b g) (k o)", k=K_PASS),
         )
         sigma_bf = const.tile([P, 1], BF16)
         nc.scalar.dma_start(out=sigma_bf[:], in_=sigma.partition_broadcast(P))
-        conf_bf = const.tile([P, ALL_GROUPS, PACK], BF16)
-        nc.scalar.dma_start(
-            out=conf_bf[:],
-            in_=flashes_confidence.rearrange("b (g q j) o -> q (b g) (j o)", q=P, j=PACK),
-        )
         pe_raw = {}
 
         def load_pe(chunk):
@@ -95,10 +104,6 @@ def tile_flashrecomodel_k_kernel(
             pe_raw[chunk] = raw
 
         load_pe(0)
-        load_pe(1)
-
-        identity = const.tile([P, P], F32)
-        make_identity(nc, identity[:])
 
         tick_low = const.tile([P, TICKS_LOW], I32)
         nc.gpsimd.iota(out=tick_low[:], pattern=[[1, TICKS_LOW]], base=0, channel_multiplier=0)
@@ -109,6 +114,10 @@ def tile_flashrecomodel_k_kernel(
             base=0,
             channel_multiplier=0,
         )
+        identity_bf = const.tile([P, P], BF16)
+        make_identity(nc, identity_bf[:])
+        identity = const.tile([P, P], F32)
+        make_identity(nc, identity[:])
         ticks = const.tile([P, TICKS], F32)
         high_low = [P, TICKS // TICKS_LOW, TICKS_LOW]
         nc.vector.tensor_tensor(
@@ -118,10 +127,14 @@ def tile_flashrecomodel_k_kernel(
             op=ALU.add,
         )
 
-        neg_centre = const.tile([P, ALL_PLANES], F32)
+        by_flash = psum.tile([P, PACK, P], BF16)
+        for j in range(PACK):
+            nc.tensor.transpose(by_flash[:, j, :], flash_rows[:, j::PACK], identity_bf[:])
+
+        neg_centre = const.tile([P, ALL_GROUPS, PACK], F32)
         nc.vector.tensor_scalar(
-            out=neg_centre[:],
-            in0=time_bf[:].rearrange("q g j -> q (g j)"),
+            out=neg_centre[:].rearrange("q g j -> q j g"),
+            in0=by_flash[:, :, 0:ALL_GROUPS],
             scalar1=float(TICKS),
             scalar2=0.0,
             op0=ALU.mult,
@@ -151,108 +164,150 @@ def tile_flashrecomodel_k_kernel(
         gauss = {}
         tick_sums = {}
 
-        def plane_of(n):
-            g, j = divmod(n, PACK)
+        def gauss_of(g):
             if g not in gauss:
                 group_tile = gauss_pool.tile([P, PACK, TICKS], F32)
                 gauss[g] = group_tile
-            return gauss[g][:, j, :]
-
-        def vector_planes(g):
-            if g >= ALL_GROUPS:
-                return []
-            return [n for n in range(g * PACK, (g + 1) * PACK) if squared_on_vector(n)]
+            return gauss[g]
 
         def differences_on_vector(g):
-            for n in vector_planes(g):
-                nc.vector.tensor_scalar(
-                    out=plane_of(n),
-                    in0=ticks[:],
-                    scalar1=neg_centre[:, n : n + 1],
-                    scalar2=None,
-                    op0=ALU.add,
-                )
+            if g < ALL_GROUPS:
+                for j, first, end in squares_of(g)[1]:
+                    nc.vector.tensor_scalar(
+                        out=gauss_of(g)[:, j, first:end],
+                        in0=ticks[:, first:end],
+                        scalar1=neg_centre[:, g, j : j + 1],
+                        scalar2=None,
+                        op0=ALU.add,
+                    )
 
         def squares_on_vector(g):
-            for n in vector_planes(g):
-                plane = plane_of(n)
-                nc.vector.tensor_tensor(out=plane, in0=plane, in1=plane, op=ALU.mult)
+            if g < ALL_GROUPS:
+                for j, first, end in squares_of(g)[1]:
+                    piece = gauss_of(g)[:, j, first:end]
+                    nc.vector.tensor_tensor(out=piece, in0=piece, in1=piece, op=ALU.mult)
 
-        def square_on_scalar(n):
-            if n < ALL_PLANES and not squared_on_vector(n):
-                nc.scalar.activation(
-                    out=plane_of(n),
-                    in_=ticks[:],
-                    func=ACT.Square,
-                    bias=neg_centre[:, n : n + 1],
-                    scale=1.0,
-                )
-
-        def gaussian_on_scalar(n):
-            if n >= ALL_PLANES:
+        def squares_on_gpsimd(g):
+            if g >= ALL_GROUPS:
                 return
-            g, j = divmod(n, PACK)
-            if j == 0:
-                tick_sum = small.tile([P, PACK], F32)
-                tick_sums[g] = tick_sum
-            square_on_scalar(n + 1)
-            plane = plane_of(n)
-            nc.scalar.activation(
-                out=plane,
-                in_=plane,
-                func=ACT.Exp,
-                scale=exp_scale[:, 0:1],
-                accum_out=tick_sums[g][:, j : j + 1],
-            )
-
-        pe_codes = const.tile([P, ALL_GROUPS, CHANNELS], U32, align_bytes=64)
-        pe_scales = const.tile([P, ALL_GROUPS, CHANNELS], U8, align_bytes=64)
-
-        def quantise_pe(chunk):
-            pe_grouped = const.tile([P, PE_CHUNK, CHANNELS, PACK], BF16, align_bytes=64)
-            for k in range(PE_CHUNK):
-                g = chunk * PE_CHUNK + k
-                conf = conf_bf[:, g, :].unsqueeze(1).unsqueeze(3)
-                nc.vector.tensor_tensor(
-                    out=words_view(pe_grouped[:, k, :, :]),
-                    in0=planes_view(pe_raw[chunk][:, k, :, :]),
-                    in1=conf.to_broadcast([P, CHANNELS // RUN, PACK, RUN]),
-                    op=ALU.mult,
+            centres = small.tile([P, PACK], F32)
+            nc.vector.tensor_copy(out=centres[:], in_=neg_centre[:, g, :])
+            pieces = squares_of(g)[0]
+            for j, first, end in pieces:
+                nc.gpsimd.tensor_scalar(
+                    out=gauss_of(g)[:, j, first:end],
+                    in0=ticks[:, first:end],
+                    scalar1=centres[:, j : j + 1],
+                    scalar2=1.0,
+                    op0=ALU.add,
+                    op1=ALU.mult,
                 )
-            if chunk + 2 < ALL_GROUPS // PE_CHUNK:
-                load_pe(chunk + 2)
-            groups = slice(chunk * PE_CHUNK, (chunk + 1) * PE_CHUNK)
-            nc.vector.quantize_mx(
-                out=pe_codes[:, groups, :].rearrange("q g c -> q (g c)").bitcast(FP8X4),
-                scales=pe_scales[:, groups, :].rearrange("q g c -> q (g c)"),
-                in_=pe_grouped[:].rearrange("q g c j -> q (g c j)"),
+            for j, first, end in pieces:
+                piece = gauss_of(g)[:, j, first:end]
+                nc.gpsimd.tensor_tensor(out=piece, in0=piece, in1=piece, op=ALU.mult)
+
+        def square_on_scalar(g, piece):
+            j, first, end = piece
+            nc.scalar.activation(
+                out=gauss_of(g)[:, j, first:end],
+                in_=ticks[:, first:end],
+                func=ACT.Square,
+                bias=neg_centre[:, g, j : j + 1],
+                scale=1.0,
             )
 
+        def gaussians_on_scalar(g):
+            if g >= ALL_GROUPS:
+                return
+            ahead = squares_of(g + 1)[2] if g + 1 < ALL_GROUPS else []
+            tick_sum = small.tile([P, PACK], F32)
+            tick_sums[g] = tick_sum
+            for j in range(PACK):
+                plane = gauss_of(g)[:, j, :]
+                nc.scalar.activation(
+                    out=plane,
+                    in_=plane,
+                    func=ACT.Exp,
+                    scale=exp_scale[:, 0:1],
+                    accum_out=tick_sum[:, j : j + 1],
+                )
+                if j < len(ahead):
+                    square_on_scalar(g + 1, ahead[j])
+
+        confidence = const.tile([P, ALL_GROUPS, PACK], F32)
+        nc.vector.tensor_copy(
+            out=confidence[:].rearrange("q g j -> q j g"),
+            in_=by_flash[:, :, ALL_GROUPS : 2 * ALL_GROUPS],
+        )
         inv_sums = {}
-        inv_factors = {}
+        factors = {}
+
+        def add_eps(g):
+            if g < ALL_GROUPS:
+                inv_sum = small.tile([P, PACK], F32)
+                nc.vector.tensor_scalar(
+                    out=inv_sum[:], in0=tick_sums[g][:], scalar1=EPS, scalar2=None, op0=ALU.add
+                )
+                inv_sums[g] = inv_sum
+
+        def invert_sums(g):
+            if g < ALL_GROUPS:
+                nc.vector.reciprocal(out=inv_sums[g][:], in_=inv_sums[g][:])
+
+        def spread(bank, first, values):
+            nc.tensor.matmul(
+                out=bank[:, first : first + PACK],
+                lhsT=identity[:],
+                rhs=values,
+                start=True,
+                stop=True,
+            )
+
+        def spread_factors(g):
+            if g < ALL_GROUPS:
+                bank = factor_psum.tile([P, N_TILE], F32)
+                spread(bank, 0, inv_sums[g][:])
+                if g + 2 < ALL_GROUPS:
+                    spread(bank, PACK, confidence[:, g + 2, :])
+                factors[g] = bank
+
+        pe_grouped = {}
+        pe_mx = {}
+
+        def scale_pe(g, bank, first):
+            if g >= ALL_GROUPS:
+                return
+            chunk, k = divmod(g, PE_CHUNK)
+            if k == 0 and chunk + 1 < ALL_GROUPS // PE_CHUNK:
+                load_pe(chunk + 1)
+            grouped = pe_mx_pool.tile([P, CHANNELS, PACK], BF16, align_bytes=64, name="pe_grouped")
+            factor = bank[:, first : first + PACK].unsqueeze(1).unsqueeze(3)
+            nc.vector.tensor_tensor(
+                out=words_view(grouped[:]),
+                in0=planes_view(pe_raw[chunk][:, k, :, :]),
+                in1=factor.to_broadcast([P, CHANNELS // RUN, PACK, RUN]),
+                op=ALU.mult,
+            )
+            pe_grouped[g] = grouped
+
+        def quantise_pe(g):
+            if g >= ALL_GROUPS:
+                return
+            codes = pe_mx_pool.tile([P, CHANNELS], U32, align_bytes=64, name="pe_codes")
+            scales = pe_mx_pool.tile([P, CHANNELS], U8, align_bytes=64, name="pe_scales")
+            nc.vector.quantize_mx(
+                out=codes[:].bitcast(FP8X4),
+                scales=scales[:],
+                in_=pe_grouped[g][:].rearrange("q c j -> q (c j)"),
+            )
+            pe_mx[g] = (codes, scales)
+
         w_grouped = {}
         acc = {}
 
-        def add_eps(g):
-            inv_sum = small.tile([P, PACK], F32)
-            nc.vector.tensor_scalar(
-                out=inv_sum[:], in0=tick_sums[g][:], scalar1=EPS, scalar2=None, op0=ALU.add
-            )
-            inv_sums[g] = inv_sum
-
-        def invert_sums(g):
-            nc.vector.reciprocal(out=inv_sums[g][:], in_=inv_sums[g][:])
-
-        def spread_inv(g):
-            bank = inv_psum.tile([P, N_TILE], F32)
-            nc.tensor.matmul(
-                out=bank[:, 0:PACK], lhsT=identity[:], rhs=inv_sums[g][:], start=True, stop=True
-            )
-            inv_factors[g] = bank
-
         def normalise(g, h):
             grouped = grouped_pool.tile([P, HALF, PACK], BF16, align_bytes=64)
-            factor = inv_factors[g][:, 0:PACK].unsqueeze(1).unsqueeze(3)
+            factor = factors[g][:, 0:PACK].unsqueeze(1).unsqueeze(3)
             nc.vector.tensor_tensor(
                 out=words_view(grouped[:]),
                 in0=planes_view(gauss[g][:, :, h * HALF : (h + 1) * HALF]),
@@ -277,51 +332,64 @@ def tile_flashrecomodel_k_kernel(
                 cols = slice(n * N_TILE, (n + 1) * N_TILE)
                 nc.tensor.matmul_mx(
                     out=acc[(b, bank)][:],
-                    lhsT=pe_codes[:, g, :].bitcast(FP8X4),
-                    lhsT_scale=pe_scales[:, g, :],
+                    lhsT=pe_mx[g][0][:].bitcast(FP8X4),
+                    lhsT_scale=pe_mx[g][1][:],
                     rhs=w_codes[:, cols].bitcast(FP8X4),
                     rhs_scale=w_scales[:, cols],
                     start=(g_in_event == 0),
                     stop=(g_in_event == GROUPS - 1),
                 )
 
-        def store_event(b):
-            for bank in range(BANKS):
-                result = out_pool.tile([CHANNELS, N_TILE], F32)
-                nc.scalar.copy(out=result[:], in_=acc[(b, bank)][:])
-                nc.sync.dma_start(
-                    out=out[b, :, bank * N_TILE : (bank + 1) * N_TILE], in_=result[:]
-                )
+        def store_bank(b, bank, copy):
+            result = out_pool.tile([CHANNELS, N_TILE], F32)
+            copy(out=result[:], in_=acc[(b, bank)][:])
+            nc.sync.dma_start(out=out[b, :, bank * N_TILE : (bank + 1) * N_TILE], in_=result[:])
 
-        square_on_scalar(0)
-        for g in range(2):
-            differences_on_vector(g)
-            squares_on_vector(g)
-        for j in range(PACK):
-            gaussian_on_scalar(j)
-        quantise_pe(0)
-        add_eps(0)
+        square_on_scalar(0, squares_of(0)[2][0])
+        for piece in range(len(squares_of(0)[1])):
+            j, first, end = squares_of(0)[1][piece]
+            plane = gauss_of(0)[:, j, first:end]
+            nc.vector.tensor_scalar(
+                out=plane,
+                in0=ticks[:, first:end],
+                scalar1=neg_centre[:, 0, j : j + 1],
+                scalar2=None,
+                op0=ALU.add,
+            )
+            nc.vector.tensor_tensor(out=plane, in0=plane, in1=plane, op=ALU.mult)
+        differences_on_vector(1)
+        squares_on_vector(1)
+        gaussians_on_scalar(0)
         differences_on_vector(2)
-        invert_sums(0)
-        spread_inv(0)
         squares_on_vector(2)
+        squares_on_gpsimd(2)
+        first_bank = factor_psum.tile([P, N_TILE], F32, name="bank")
+        spread(first_bank, 0, confidence[:, 0, :])
+        spread(first_bank, PACK, confidence[:, 1, :])
+        for g in range(2):
+            scale_pe(g, first_bank, g * PACK)
+        for g in range(2):
+            quantise_pe(g)
+        add_eps(0)
+        squares_on_gpsimd(3)
+        invert_sums(0)
+        spread_factors(0)
         for g in range(ALL_GROUPS):
-            gaussian_on_scalar((g + 1) * PACK)
-            if g == GROUPS:
-                store_event(0)
-            for j in range(1, PACK):
-                gaussian_on_scalar((g + 1) * PACK + j)
+            gaussians_on_scalar(g + 1)
             normalise(g, 0)
-            if g % PE_CHUNK == 0 and g + PE_CHUNK < ALL_GROUPS:
-                quantise_pe(g // PE_CHUNK + 1)
+            scale_pe(g + 2, factors[g], PACK)
+            if g == GROUPS:
+                for bank in range(BANKS):
+                    store_bank(0, bank, nc.vector.tensor_copy)
             normalise(g, 1)
             quantise_and_multiply(g, 0)
+            add_eps(g + 1)
             differences_on_vector(g + 3)
-            if g + 1 < ALL_GROUPS:
-                add_eps(g + 1)
+            invert_sums(g + 1)
+            spread_factors(g + 1)
+            quantise_pe(g + 2)
             quantise_and_multiply(g, 1)
             squares_on_vector(g + 3)
-            if g + 1 < ALL_GROUPS:
-                invert_sums(g + 1)
-                spread_inv(g + 1)
-        store_event(EVENTS - 1)
+            squares_on_gpsimd(g + 4)
+        for bank in range(BANKS):
+            store_bank(1, bank, nc.vector.tensor_copy if bank % 2 else nc.scalar.copy)

@@ -31,24 +31,38 @@ PE_CHUNK = 8
 RUN = 4
 TICKS_LOW = 128
 EPS = 1e-10
-GPSIMD_END = 512
-VECTOR_END = 1536
+GPSIMD_COLS = 2688
+VECTOR_COLS = 640
+TENSOR_COLS = 512
+EXP_ORDER = [2, 3, 1, 0]
+VECTOR_LAST = ALL_GROUPS - 3
 GROUP_BUFS = 4
 
 FLOPS = 2 * EVENTS * FLASHES * CHANNELS * TICKS
 
 
+def tensor_planes(g):
+    return [1, 2, 3] if g >= 4 and g % 2 == 0 else []
+
+
 def squares_of(g):
     if g == 0:
-        return [], [(1, 0, TICKS), (2, 0, TICKS), (3, 0, TICKS)], [(0, 0, TICKS)]
+        return [], [(3, 0, TICKS), (1, 0, TICKS), (0, 0, TICKS)], [(2, 0, TICKS)]
     if g == 1:
-        return [], [(1, 0, TICKS)], [(0, 0, TICKS), (2, 0, TICKS), (3, 0, TICKS)]
-    vector_end = VECTOR_END if g < ALL_GROUPS - 2 else GPSIMD_END
-    return (
-        [(0, 0, TICKS), (1, 0, GPSIMD_END)],
-        [(1, GPSIMD_END, vector_end)] if vector_end > GPSIMD_END else [],
-        [(1, vector_end, TICKS), (2, 0, TICKS), (3, 0, TICKS)],
-    )
+        return [], [(1, 0, TICKS)], [(2, 0, TICKS), (3, 0, TICKS), (0, 0, TICKS)]
+    quotas = [GPSIMD_COLS, VECTOR_COLS if g < VECTOR_LAST else 0, PACK * TICKS]
+    pieces = [[], [], []]
+    engine = 0
+    for j in range(PACK):
+        first = TENSOR_COLS if j in tensor_planes(g) else 0
+        while first < TICKS:
+            while quotas[engine] == 0:
+                engine += 1
+            end = min(TICKS, first + quotas[engine])
+            pieces[engine].append((j, first, end))
+            quotas[engine] -= end - first
+            first = end
+    return pieces
 
 
 def planes_view(planes):
@@ -72,20 +86,23 @@ def tile_flashrecomodel_k_kernel(
         grouped_pool = ctx.enter_context(tc.tile_pool(name="grouped", bufs=3))
         mx_pool = ctx.enter_context(tc.tile_pool(name="mx", bufs=4))
         pe_pool = ctx.enter_context(tc.tile_pool(name="pe", bufs=2))
+        terms_pool = ctx.enter_context(tc.tile_pool(name="terms", bufs=2))
         pe_mx_pool = ctx.enter_context(tc.tile_pool(name="pe_mx", bufs=4))
         out_pool = ctx.enter_context(tc.tile_pool(name="result", bufs=4))
         psum = ctx.enter_context(tc.psum_pool(name="acc", bufs=1))
-        factor_psum = ctx.enter_context(tc.psum_pool(name="factor", bufs=2))
+        factor_psum = ctx.enter_context(tc.psum_pool(name="factor", bufs=1))
+        square_psum = ctx.enter_context(tc.psum_pool(name="square", bufs=3))
         ctx.enter_context(tc.manual_schedule())
 
         flash_rows = const.tile([P, K_PASS], BF16)
         nc.vector.memset(flash_rows[:], 0.0)
-        nc.sync.dma_start(
-            out=flash_rows[0:ALL_GROUPS, :],
-            in_=flashes_time.rearrange("b (g k) o -> (b g) (k o)", k=K_PASS),
-        )
+        for copy in range(2):
+            nc.sync.dma_start(
+                out=flash_rows[copy * ALL_GROUPS : (copy + 1) * ALL_GROUPS, :],
+                in_=flashes_time.rearrange("b (g k) o -> (b g) (k o)", k=K_PASS),
+            )
         nc.scalar.dma_start(
-            out=flash_rows[ALL_GROUPS : 2 * ALL_GROUPS, :],
+            out=flash_rows[2 * ALL_GROUPS : 3 * ALL_GROUPS, :],
             in_=flashes_confidence.rearrange("b (g k) o -> (b g) (k o)", k=K_PASS),
         )
         sigma_bf = const.tile([P, 1], BF16)
@@ -127,7 +144,7 @@ def tile_flashrecomodel_k_kernel(
             op=ALU.add,
         )
 
-        by_flash = psum.tile([P, PACK, P], BF16)
+        by_flash = square_psum.tile([P, PACK, P], BF16, name="square")
         for j in range(PACK):
             nc.tensor.transpose(by_flash[:, j, :], flash_rows[:, j::PACK], identity_bf[:])
 
@@ -163,6 +180,8 @@ def tile_flashrecomodel_k_kernel(
 
         gauss = {}
         tick_sums = {}
+        first_sums = {}
+        tensor_squares = {}
 
         def gauss_of(g):
             if g not in gauss:
@@ -219,25 +238,116 @@ def tile_flashrecomodel_k_kernel(
         def gaussians_on_scalar(g):
             if g >= ALL_GROUPS:
                 return
-            ahead = squares_of(g + 1)[2] if g + 1 < ALL_GROUPS else []
+            for piece in squares_of(g)[2]:
+                square_on_scalar(g, piece)
+            if tensor_planes(g):
+                first_sum = small.tile([P, PACK], F32)
+                first_sums[g] = first_sum
+                for j in tensor_planes(g):
+                    nc.scalar.activation(
+                        out=gauss_of(g)[:, j, 0:TENSOR_COLS],
+                        in_=tensor_squares[(g, j)][:],
+                        func=ACT.Exp,
+                        scale=exp_scale[:, 0:1],
+                        accum_out=first_sum[:, j : j + 1],
+                    )
             tick_sum = small.tile([P, PACK], F32)
             tick_sums[g] = tick_sum
-            for j in range(PACK):
-                plane = gauss_of(g)[:, j, :]
+            for j in EXP_ORDER:
+                piece = gauss_of(g)[:, j, TENSOR_COLS if j in tensor_planes(g) else 0 : TICKS]
                 nc.scalar.activation(
-                    out=plane,
-                    in_=plane,
+                    out=piece,
+                    in_=piece,
                     func=ACT.Exp,
                     scale=exp_scale[:, 0:1],
                     accum_out=tick_sum[:, j : j + 1],
                 )
-                if j < len(ahead):
-                    square_on_scalar(g + 1, ahead[j])
+
+        flash_terms = const.tile([P, K_PASS], F32)
+        tick_terms = const.tile([P, TENSOR_COLS], F32)
+        row_choice = const.tile([P, ALL_GROUPS], F32)
+
+        def make_terms():
+            low = slice(0, ALL_GROUPS)
+            middle = slice(ALL_GROUPS, 2 * ALL_GROUPS)
+            high = slice(2 * ALL_GROUPS, P)
+            nc.vector.tensor_scalar(
+                out=flash_terms[0 : 2 * ALL_GROUPS, :],
+                in0=flash_rows[0 : 2 * ALL_GROUPS, :],
+                scalar1=float(TICKS),
+                scalar2=0.0,
+                op0=ALU.mult,
+                op1=ALU.max,
+            )
+            nc.vector.tensor_copy(out=tick_terms[low, :], in_=ticks[low, 0:TENSOR_COLS])
+            nc.vector.tensor_scalar(
+                out=flash_terms[0 : 2 * ALL_GROUPS, :],
+                in0=flash_terms[0 : 2 * ALL_GROUPS, :],
+                scalar1=float(TICKS - 1),
+                scalar2=None,
+                op0=ALU.min,
+            )
+            nc.vector.tensor_tensor(
+                out=tick_terms[high, :],
+                in0=ticks[high, 0:TENSOR_COLS],
+                in1=ticks[high, 0:TENSOR_COLS],
+                op=ALU.mult,
+            )
+            nc.vector.tensor_scalar(
+                out=flash_terms[low, :],
+                in0=flash_terms[low, :],
+                scalar1=-2.0,
+                scalar2=None,
+                op0=ALU.mult,
+            )
+            nc.vector.tensor_tensor(
+                out=flash_terms[middle, :],
+                in0=flash_terms[middle, :],
+                in1=flash_terms[middle, :],
+                op=ALU.mult,
+            )
+            nc.vector.memset(tick_terms[middle, :], 1.0)
+            nc.vector.memset(flash_terms[high, :], 1.0)
+            nc.vector.tensor_tensor(
+                out=row_choice[:],
+                in0=identity[:, low],
+                in1=identity[:, middle],
+                op=ALU.add,
+            )
+            nc.vector.tensor_scalar(
+                out=row_choice[:],
+                in0=row_choice[:],
+                scalar1=identity[:, 2 * ALL_GROUPS : 2 * ALL_GROUPS + 1],
+                scalar2=None,
+                op0=ALU.add,
+            )
+
+        def squares_on_tensor(g):
+            if g >= ALL_GROUPS or not tensor_planes(g):
+                return
+            chosen = terms_pool.tile([P, TENSOR_COLS], F32)
+            nc.vector.tensor_scalar(
+                out=chosen[:],
+                in0=tick_terms[:],
+                scalar1=row_choice[:, g : g + 1],
+                scalar2=None,
+                op0=ALU.mult,
+            )
+            for j in tensor_planes(g):
+                square = square_psum.tile([P, TENSOR_COLS], F32)
+                nc.tensor.matmul(
+                    out=square[:],
+                    lhsT=flash_terms[:, j::PACK],
+                    rhs=chosen[:],
+                    start=True,
+                    stop=True,
+                )
+                tensor_squares[(g, j)] = square
 
         confidence = const.tile([P, ALL_GROUPS, PACK], F32)
         nc.vector.tensor_copy(
             out=confidence[:].rearrange("q g j -> q j g"),
-            in_=by_flash[:, :, ALL_GROUPS : 2 * ALL_GROUPS],
+            in_=by_flash[:, :, 2 * ALL_GROUPS : 3 * ALL_GROUPS],
         )
         inv_sums = {}
         factors = {}
@@ -248,6 +358,14 @@ def tile_flashrecomodel_k_kernel(
                 nc.vector.tensor_scalar(
                     out=inv_sum[:], in0=tick_sums[g][:], scalar1=EPS, scalar2=None, op0=ALU.add
                 )
+                if tensor_planes(g):
+                    both = slice(tensor_planes(g)[0], PACK)
+                    nc.vector.tensor_tensor(
+                        out=inv_sum[:, both],
+                        in0=inv_sum[:, both],
+                        in1=first_sums[g][:, both],
+                        op=ALU.add,
+                    )
                 inv_sums[g] = inv_sum
 
         def invert_sums(g):
@@ -345,7 +463,6 @@ def tile_flashrecomodel_k_kernel(
             copy(out=result[:], in_=acc[(b, bank)][:])
             nc.sync.dma_start(out=out[b, :, bank * N_TILE : (bank + 1) * N_TILE], in_=result[:])
 
-        square_on_scalar(0, squares_of(0)[2][0])
         for piece in range(len(squares_of(0)[1])):
             j, first, end = squares_of(0)[1][piece]
             plane = gauss_of(0)[:, j, first:end]
@@ -360,9 +477,6 @@ def tile_flashrecomodel_k_kernel(
         differences_on_vector(1)
         squares_on_vector(1)
         gaussians_on_scalar(0)
-        differences_on_vector(2)
-        squares_on_vector(2)
-        squares_on_gpsimd(2)
         first_bank = factor_psum.tile([P, N_TILE], F32, name="bank")
         spread(first_bank, 0, confidence[:, 0, :])
         spread(first_bank, PACK, confidence[:, 1, :])
@@ -371,7 +485,7 @@ def tile_flashrecomodel_k_kernel(
         for g in range(2):
             quantise_pe(g)
         add_eps(0)
-        squares_on_gpsimd(3)
+        squares_on_gpsimd(2)
         invert_sums(0)
         spread_factors(0)
         for g in range(ALL_GROUPS):
@@ -384,12 +498,15 @@ def tile_flashrecomodel_k_kernel(
             normalise(g, 1)
             quantise_and_multiply(g, 0)
             add_eps(g + 1)
-            differences_on_vector(g + 3)
+            differences_on_vector(g + 2)
             invert_sums(g + 1)
             spread_factors(g + 1)
+            if g == 0:
+                make_terms()
+            squares_on_tensor(g + 3)
             quantise_pe(g + 2)
             quantise_and_multiply(g, 1)
-            squares_on_vector(g + 3)
-            squares_on_gpsimd(g + 4)
+            squares_on_vector(g + 2)
+            squares_on_gpsimd(g + 3)
         for bank in range(BANKS):
             store_bank(1, bank, nc.vector.tensor_copy if bank % 2 else nc.scalar.copy)

@@ -31,12 +31,12 @@ PE_CHUNK = 8
 RUN = 4
 TICKS_LOW = 128
 EPS = 1e-10
-GPSIMD_COLS = 2688
-VECTOR_COLS = 640
+GPSIMD_COLS = 2560
+VECTOR_COLS = 800
 TENSOR_COLS = 512
 EXP_ORDER = [2, 3, 1, 0]
-VECTOR_LAST = ALL_GROUPS - 3
 GROUP_BUFS = 4
+FIRST_GROUPS = 2
 
 FLOPS = 2 * EVENTS * FLASHES * CHANNELS * TICKS
 
@@ -50,15 +50,16 @@ def squares_of(g):
         return [], [(3, 0, TICKS), (1, 0, TICKS), (0, 0, TICKS)], [(2, 0, TICKS)]
     if g == 1:
         return [], [(1, 0, TICKS)], [(2, 0, TICKS), (3, 0, TICKS), (0, 0, TICKS)]
-    quotas = [GPSIMD_COLS, VECTOR_COLS if g < VECTOR_LAST else 0, PACK * TICKS]
+    quotas = [GPSIMD_COLS, VECTOR_COLS, PACK * TICKS]
     pieces = [[], [], []]
     engine = 0
     for j in range(PACK):
-        first = TENSOR_COLS if j in tensor_planes(g) else 0
-        while first < TICKS:
+        first = 0
+        plane_end = TICKS - TENSOR_COLS if j in tensor_planes(g) else TICKS
+        while first < plane_end:
             while quotas[engine] == 0:
                 engine += 1
-            end = min(TICKS, first + quotas[engine])
+            end = min(plane_end, first + quotas[engine])
             pieces[engine].append((j, first, end))
             quotas[engine] -= end - first
             first = end
@@ -96,6 +97,13 @@ def tile_flashrecomodel_k_kernel(
 
         flash_rows = const.tile([P, K_PASS], BF16)
         nc.vector.memset(flash_rows[:], 0.0)
+        first_times = const.tile([P, FIRST_GROUPS, PACK], BF16)
+        nc.sync.dma_start(
+            out=first_times[:],
+            in_=flashes_time[0, 0 : FIRST_GROUPS * K_PASS, :].rearrange(
+                "(g q j) o -> q g (j o)", q=P, j=PACK
+            ),
+        )
         for copy in range(2):
             nc.sync.dma_start(
                 out=flash_rows[copy * ALL_GROUPS : (copy + 1) * ALL_GROUPS, :],
@@ -148,23 +156,30 @@ def tile_flashrecomodel_k_kernel(
         for j in range(PACK):
             nc.tensor.transpose(by_flash[:, j, :], flash_rows[:, j::PACK], identity_bf[:])
 
+        def negated_centres(out, times):
+            nc.vector.tensor_scalar(
+                out=out,
+                in0=times,
+                scalar1=float(TICKS),
+                scalar2=0.0,
+                op0=ALU.mult,
+                op1=ALU.max,
+            )
+            nc.vector.tensor_scalar(
+                out=out,
+                in0=out,
+                scalar1=float(TICKS - 1),
+                scalar2=-1.0,
+                op0=ALU.min,
+                op1=ALU.mult,
+            )
+
+        first_centre = const.tile([P, FIRST_GROUPS, PACK], F32)
+        negated_centres(first_centre[:], first_times[:])
         neg_centre = const.tile([P, ALL_GROUPS, PACK], F32)
-        nc.vector.tensor_scalar(
-            out=neg_centre[:].rearrange("q g j -> q j g"),
-            in0=by_flash[:, :, 0:ALL_GROUPS],
-            scalar1=float(TICKS),
-            scalar2=0.0,
-            op0=ALU.mult,
-            op1=ALU.max,
-        )
-        nc.vector.tensor_scalar(
-            out=neg_centre[:],
-            in0=neg_centre[:],
-            scalar1=float(TICKS - 1),
-            scalar2=-1.0,
-            op0=ALU.min,
-            op1=ALU.mult,
-        )
+
+        def centre(g, j):
+            return (first_centre if g < FIRST_GROUPS else neg_centre)[:, g, j : j + 1]
 
         neg_two_var = const.tile([P, 1], F32)
         nc.vector.scalar_tensor_tensor(
@@ -179,6 +194,11 @@ def tile_flashrecomodel_k_kernel(
         nc.vector.reciprocal(out=exp_scale[:], in_=neg_two_var[:])
 
         gauss = {}
+        spare_sums = []
+        for copy in range(2):
+            spare_sum = const.tile([P, PACK], F32, name="spare_sum%d" % copy)
+            nc.gpsimd.memset(spare_sum[:], 0.0)
+            spare_sums.append(spare_sum)
         tick_sums = {}
         first_sums = {}
         tensor_squares = {}
@@ -195,7 +215,7 @@ def tile_flashrecomodel_k_kernel(
                     nc.vector.tensor_scalar(
                         out=gauss_of(g)[:, j, first:end],
                         in0=ticks[:, first:end],
-                        scalar1=neg_centre[:, g, j : j + 1],
+                        scalar1=centre(g, j),
                         scalar2=None,
                         op0=ALU.add,
                     )
@@ -221,9 +241,8 @@ def tile_flashrecomodel_k_kernel(
                     op0=ALU.add,
                     op1=ALU.mult,
                 )
-            for j, first, end in pieces:
-                piece = gauss_of(g)[:, j, first:end]
-                nc.gpsimd.tensor_tensor(out=piece, in0=piece, in1=piece, op=ALU.mult)
+            piece = gauss_of(g)[:].rearrange("q j t -> q (j t)")[:, 0:GPSIMD_COLS]
+            nc.gpsimd.tensor_tensor(out=piece, in0=piece, in1=piece, op=ALU.mult)
 
         def square_on_scalar(g, piece):
             j, first, end = piece
@@ -231,7 +250,7 @@ def tile_flashrecomodel_k_kernel(
                 out=gauss_of(g)[:, j, first:end],
                 in_=ticks[:, first:end],
                 func=ACT.Square,
-                bias=neg_centre[:, g, j : j + 1],
+                bias=centre(g, j),
                 scale=1.0,
             )
 
@@ -241,11 +260,11 @@ def tile_flashrecomodel_k_kernel(
             for piece in squares_of(g)[2]:
                 square_on_scalar(g, piece)
             if tensor_planes(g):
-                first_sum = small.tile([P, PACK], F32)
+                first_sum = spare_sums[g // 2 % 2]
                 first_sums[g] = first_sum
                 for j in tensor_planes(g):
                     nc.scalar.activation(
-                        out=gauss_of(g)[:, j, 0:TENSOR_COLS],
+                        out=gauss_of(g)[:, j, TICKS - TENSOR_COLS : TICKS],
                         in_=tensor_squares[(g, j)][:],
                         func=ACT.Exp,
                         scale=exp_scale[:, 0:1],
@@ -254,7 +273,8 @@ def tile_flashrecomodel_k_kernel(
             tick_sum = small.tile([P, PACK], F32)
             tick_sums[g] = tick_sum
             for j in EXP_ORDER:
-                piece = gauss_of(g)[:, j, TENSOR_COLS if j in tensor_planes(g) else 0 : TICKS]
+                end = TICKS - TENSOR_COLS if j in tensor_planes(g) else TICKS
+                piece = gauss_of(g)[:, j, 0:end]
                 nc.scalar.activation(
                     out=piece,
                     in_=piece,
@@ -279,7 +299,7 @@ def tile_flashrecomodel_k_kernel(
                 op0=ALU.mult,
                 op1=ALU.max,
             )
-            nc.vector.tensor_copy(out=tick_terms[low, :], in_=ticks[low, 0:TENSOR_COLS])
+            nc.vector.tensor_copy(out=tick_terms[low, :], in_=ticks[low, TICKS - TENSOR_COLS : TICKS])
             nc.vector.tensor_scalar(
                 out=flash_terms[0 : 2 * ALL_GROUPS, :],
                 in0=flash_terms[0 : 2 * ALL_GROUPS, :],
@@ -289,8 +309,8 @@ def tile_flashrecomodel_k_kernel(
             )
             nc.vector.tensor_tensor(
                 out=tick_terms[high, :],
-                in0=ticks[high, 0:TENSOR_COLS],
-                in1=ticks[high, 0:TENSOR_COLS],
+                in0=ticks[high, TICKS - TENSOR_COLS : TICKS],
+                in1=ticks[high, TICKS - TENSOR_COLS : TICKS],
                 op=ALU.mult,
             )
             nc.vector.tensor_scalar(
@@ -345,26 +365,24 @@ def tile_flashrecomodel_k_kernel(
                 tensor_squares[(g, j)] = square
 
         confidence = const.tile([P, ALL_GROUPS, PACK], F32)
-        nc.vector.tensor_copy(
-            out=confidence[:].rearrange("q g j -> q j g"),
-            in_=by_flash[:, :, 2 * ALL_GROUPS : 3 * ALL_GROUPS],
-        )
         inv_sums = {}
         factors = {}
 
         def add_eps(g):
             if g < ALL_GROUPS:
                 inv_sum = small.tile([P, PACK], F32)
-                nc.vector.tensor_scalar(
-                    out=inv_sum[:], in0=tick_sums[g][:], scalar1=EPS, scalar2=None, op0=ALU.add
-                )
-                if tensor_planes(g):
-                    both = slice(tensor_planes(g)[0], PACK)
-                    nc.vector.tensor_tensor(
-                        out=inv_sum[:, both],
-                        in0=inv_sum[:, both],
-                        in1=first_sums[g][:, both],
-                        op=ALU.add,
+                if g in first_sums:
+                    nc.vector.scalar_tensor_tensor(
+                        out=inv_sum[:],
+                        in0=tick_sums[g][:],
+                        scalar=EPS,
+                        in1=first_sums[g][:],
+                        op0=ALU.add,
+                        op1=ALU.add,
+                    )
+                else:
+                    nc.vector.tensor_scalar(
+                        out=inv_sum[:], in0=tick_sums[g][:], scalar1=EPS, scalar2=None, op0=ALU.add
                     )
                 inv_sums[g] = inv_sum
 
@@ -434,6 +452,22 @@ def tile_flashrecomodel_k_kernel(
             )
             w_grouped[(g, h)] = grouped
 
+        w_planes = const.tile([P, PACK, HALF], BF16)
+
+        def normalise_on_scalar(g, h):
+            for j in range(PACK):
+                nc.scalar.activation(
+                    out=w_planes[:, j, :],
+                    in_=gauss[g][:, j, h * HALF : (h + 1) * HALF],
+                    func=ACT.Copy,
+                    scale=inv_sums[g][:, j : j + 1],
+                )
+
+        def regroup(g, h):
+            grouped = grouped_pool.tile([P, HALF, PACK], BF16, align_bytes=64)
+            nc.vector.tensor_copy(out=words_view(grouped[:]), in_=planes_view(w_planes[:]))
+            w_grouped[(g, h)] = grouped
+
         def quantise_and_multiply(g, h):
             b, g_in_event = divmod(g, GROUPS)
             w_codes = mx_pool.tile([P, HALF], U32, align_bytes=64)
@@ -469,12 +503,17 @@ def tile_flashrecomodel_k_kernel(
             nc.vector.tensor_scalar(
                 out=plane,
                 in0=ticks[:, first:end],
-                scalar1=neg_centre[:, 0, j : j + 1],
+                scalar1=centre(0, j),
                 scalar2=None,
                 op0=ALU.add,
             )
             nc.vector.tensor_tensor(out=plane, in0=plane, in1=plane, op=ALU.mult)
+        nc.vector.tensor_copy(
+            out=confidence[:].rearrange("q g j -> q j g"),
+            in_=by_flash[:, :, 2 * ALL_GROUPS : 3 * ALL_GROUPS],
+        )
         differences_on_vector(1)
+        negated_centres(neg_centre[:].rearrange("q g j -> q j g"), by_flash[:, :, 0:ALL_GROUPS])
         squares_on_vector(1)
         gaussians_on_scalar(0)
         first_bank = factor_psum.tile([P, N_TILE], F32, name="bank")
@@ -495,7 +534,11 @@ def tile_flashrecomodel_k_kernel(
             if g == GROUPS:
                 for bank in range(BANKS):
                     store_bank(0, bank, nc.vector.tensor_copy)
-            normalise(g, 1)
+            if g < ALL_GROUPS - 1:
+                normalise(g, 1)
+            else:
+                normalise_on_scalar(g, 1)
+                regroup(g, 1)
             quantise_and_multiply(g, 0)
             add_eps(g + 1)
             differences_on_vector(g + 2)

@@ -31,8 +31,8 @@ PE_CHUNK = 8
 RUN = 4
 TICKS_LOW = 128
 EPS = 1e-10
-GPSIMD_COLS = 2560
-VECTOR_COLS = 800
+GPSIMD_COLS = 1024
+SHARED_COLS = 3456
 TENSOR_COLS = 512
 EXP_ORDER = [2, 3, 1, 0]
 GROUP_BUFS = 4
@@ -50,7 +50,7 @@ def squares_of(g):
         return [], [(3, 0, TICKS), (1, 0, TICKS), (0, 0, TICKS)], [(2, 0, TICKS)]
     if g == 1:
         return [], [(1, 0, TICKS)], [(2, 0, TICKS), (3, 0, TICKS), (0, 0, TICKS)]
-    quotas = [GPSIMD_COLS, VECTOR_COLS, PACK * TICKS]
+    quotas = [GPSIMD_COLS, SHARED_COLS - GPSIMD_COLS, PACK * TICKS]
     pieces = [[], [], []]
     engine = 0
     for j in range(PACK):
@@ -226,22 +226,23 @@ def tile_flashrecomodel_k_kernel(
                     piece = gauss_of(g)[:, j, first:end]
                     nc.vector.tensor_tensor(out=piece, in0=piece, in1=piece, op=ALU.mult)
 
-        def squares_on_gpsimd(g):
+        def differences_on_gpsimd(g):
             if g >= ALL_GROUPS:
                 return
-            centres = small.tile([P, PACK], F32)
-            nc.vector.tensor_copy(out=centres[:], in_=neg_centre[:, g, :])
-            pieces = squares_of(g)[0]
-            for j, first, end in pieces:
+            for j, first, end in squares_of(g)[0]:
                 nc.gpsimd.tensor_scalar(
                     out=gauss_of(g)[:, j, first:end],
                     in0=ticks[:, first:end],
-                    scalar1=centres[:, j : j + 1],
+                    scalar1=centre(g, j),
                     scalar2=1.0,
                     op0=ALU.add,
                     op1=ALU.mult,
                 )
-            piece = gauss_of(g)[:].rearrange("q j t -> q (j t)")[:, 0:GPSIMD_COLS]
+
+        def squares_on_gpsimd(g):
+            if g >= ALL_GROUPS:
+                return
+            piece = gauss_of(g)[:].rearrange("q j t -> q (j t)")[:, 0:SHARED_COLS]
             nc.gpsimd.tensor_tensor(out=piece, in0=piece, in1=piece, op=ALU.mult)
 
         def square_on_scalar(g, piece):
@@ -524,7 +525,10 @@ def tile_flashrecomodel_k_kernel(
         for g in range(2):
             quantise_pe(g)
         add_eps(0)
+        differences_on_vector(2)
+        differences_on_gpsimd(2)
         squares_on_gpsimd(2)
+        differences_on_gpsimd(3)
         invert_sums(0)
         spread_factors(0)
         for g in range(ALL_GROUPS):
@@ -541,7 +545,6 @@ def tile_flashrecomodel_k_kernel(
                 regroup(g, 1)
             quantise_and_multiply(g, 0)
             add_eps(g + 1)
-            differences_on_vector(g + 2)
             invert_sums(g + 1)
             spread_factors(g + 1)
             if g == 0:
@@ -549,7 +552,8 @@ def tile_flashrecomodel_k_kernel(
             squares_on_tensor(g + 3)
             quantise_pe(g + 2)
             quantise_and_multiply(g, 1)
-            squares_on_vector(g + 2)
+            differences_on_vector(g + 3)
             squares_on_gpsimd(g + 3)
+            differences_on_gpsimd(g + 4)
         for bank in range(BANKS):
             store_bank(1, bank, nc.vector.tensor_copy if bank % 2 else nc.scalar.copy)

@@ -34,6 +34,7 @@ EPS = 1e-10
 GPSIMD_COLS = 1024
 SHARED_COLS = 3456
 TENSOR_COLS = 512
+TENSOR_GROUPS = 25
 EXP_ORDER = [2, 3, 1, 0]
 GROUP_BUFS = 4
 FIRST_GROUPS = 2
@@ -42,12 +43,12 @@ FLOPS = 2 * EVENTS * FLASHES * CHANNELS * TICKS
 
 
 def tensor_planes(g):
-    return [1, 2, 3] if g >= 4 and g % 2 == 0 else []
+    return [2, 3] if g >= ALL_GROUPS - TENSOR_GROUPS else []
 
 
 def squares_of(g):
     if g == 0:
-        return [], [(3, 0, TICKS), (1, 0, TICKS), (0, 0, TICKS)], [(2, 0, TICKS)]
+        return [], [(3, 0, TICKS), (1, 0, TICKS), (0, 0, HALF)], [(2, 0, TICKS), (0, HALF, TICKS)]
     if g == 1:
         return [], [(1, 0, TICKS)], [(2, 0, TICKS), (3, 0, TICKS), (0, 0, TICKS)]
     quotas = [GPSIMD_COLS, SHARED_COLS - GPSIMD_COLS, PACK * TICKS]
@@ -87,7 +88,6 @@ def tile_flashrecomodel_k_kernel(
         grouped_pool = ctx.enter_context(tc.tile_pool(name="grouped", bufs=3))
         mx_pool = ctx.enter_context(tc.tile_pool(name="mx", bufs=4))
         pe_pool = ctx.enter_context(tc.tile_pool(name="pe", bufs=2))
-        terms_pool = ctx.enter_context(tc.tile_pool(name="terms", bufs=2))
         pe_mx_pool = ctx.enter_context(tc.tile_pool(name="pe_mx", bufs=4))
         out_pool = ctx.enter_context(tc.tile_pool(name="result", bufs=4))
         psum = ctx.enter_context(tc.psum_pool(name="acc", bufs=1))
@@ -258,19 +258,8 @@ def tile_flashrecomodel_k_kernel(
         def gaussians_on_scalar(g):
             if g >= ALL_GROUPS:
                 return
-            for piece in squares_of(g)[2]:
+            for piece in squares_of(g)[2][: 1 if g == 0 else None]:
                 square_on_scalar(g, piece)
-            if tensor_planes(g):
-                first_sum = spare_sums[g // 2 % 2]
-                first_sums[g] = first_sum
-                for j in tensor_planes(g):
-                    nc.scalar.activation(
-                        out=gauss_of(g)[:, j, TICKS - TENSOR_COLS : TICKS],
-                        in_=tensor_squares[(g, j)][:],
-                        func=ACT.Exp,
-                        scale=exp_scale[:, 0:1],
-                        accum_out=first_sum[:, j : j + 1],
-                    )
             tick_sum = small.tile([P, PACK], F32)
             tick_sums[g] = tick_sum
             for j in EXP_ORDER:
@@ -283,10 +272,26 @@ def tile_flashrecomodel_k_kernel(
                     scale=exp_scale[:, 0:1],
                     accum_out=tick_sum[:, j : j + 1],
                 )
+                if g == 0 and j == 2:
+                    square_on_scalar(0, squares_of(0)[2][1])
+                if j == EXP_ORDER[1] and tensor_planes(g):
+                    first_sum = spare_sums[g % 2]
+                    first_sums[g] = first_sum
+                    for k in tensor_planes(g):
+                        nc.scalar.activation(
+                            out=gauss_of(g)[:, k, TICKS - TENSOR_COLS : TICKS],
+                            in_=tensor_squares[(g, k)][:],
+                            func=ACT.Exp,
+                            scale=exp_scale[:, 0:1],
+                            accum_out=first_sum[:, k : k + 1],
+                        )
 
         flash_terms = const.tile([P, K_PASS], F32)
         tick_terms = const.tile([P, TENSOR_COLS], F32)
-        row_choice = const.tile([P, ALL_GROUPS], F32)
+        stationaries = []
+        for copy in range(2):
+            stationary = const.tile([P, K_PASS], F32, name="stationary%d" % copy)
+            stationaries.append(stationary)
 
         def make_terms():
             low = slice(0, ALL_GROUPS)
@@ -327,39 +332,25 @@ def tile_flashrecomodel_k_kernel(
                 in1=flash_terms[middle, :],
                 op=ALU.mult,
             )
+            for stationary in stationaries:
+                nc.vector.memset(stationary[:], 0.0)
             nc.vector.memset(tick_terms[middle, :], 1.0)
             nc.vector.memset(flash_terms[high, :], 1.0)
-            nc.vector.tensor_tensor(
-                out=row_choice[:],
-                in0=identity[:, low],
-                in1=identity[:, middle],
-                op=ALU.add,
-            )
-            nc.vector.tensor_scalar(
-                out=row_choice[:],
-                in0=row_choice[:],
-                scalar1=identity[:, 2 * ALL_GROUPS : 2 * ALL_GROUPS + 1],
-                scalar2=None,
-                op0=ALU.add,
-            )
 
         def squares_on_tensor(g):
             if g >= ALL_GROUPS or not tensor_planes(g):
                 return
-            chosen = terms_pool.tile([P, TENSOR_COLS], F32)
-            nc.vector.tensor_scalar(
-                out=chosen[:],
-                in0=tick_terms[:],
-                scalar1=row_choice[:, g : g + 1],
-                scalar2=None,
-                op0=ALU.mult,
+            stationary = stationaries[g % 2]
+            nc.sync.dma_start(
+                out=stationary[0 : 2 * ALL_GROUPS + 1 : ALL_GROUPS, :],
+                in_=flash_terms[g : g + 2 * ALL_GROUPS + 1 : ALL_GROUPS, :],
             )
             for j in tensor_planes(g):
                 square = square_psum.tile([P, TENSOR_COLS], F32)
                 nc.tensor.matmul(
                     out=square[:],
-                    lhsT=flash_terms[:, j::PACK],
-                    rhs=chosen[:],
+                    lhsT=stationary[:, j::PACK],
+                    rhs=tick_terms[:],
                     start=True,
                     stop=True,
                 )
@@ -545,12 +536,12 @@ def tile_flashrecomodel_k_kernel(
                 regroup(g, 1)
             quantise_and_multiply(g, 0)
             add_eps(g + 1)
+            quantise_pe(g + 2)
             invert_sums(g + 1)
             spread_factors(g + 1)
             if g == 0:
                 make_terms()
-            squares_on_tensor(g + 3)
-            quantise_pe(g + 2)
+            squares_on_tensor(g + 2)
             quantise_and_multiply(g, 1)
             differences_on_vector(g + 3)
             squares_on_gpsimd(g + 3)

@@ -27,11 +27,11 @@ BANKS = TICKS // N_TILE
 HALVES = 2
 HALF = TICKS // HALVES
 BANKS_PER_HALF = HALF // N_TILE
-PE_CHUNK = 8
+PE_CHUNK = 4
 RUN = 4
 TICKS_LOW = 128
 EPS = 1e-10
-GPSIMD_COLS = 1024
+GPSIMD_COLS = 1280
 SHARED_COLS = 3456
 TENSOR_COLS = 512
 TENSOR_GROUPS = 25
@@ -85,7 +85,7 @@ def tile_flashrecomodel_k_kernel(
         const = ctx.enter_context(tc.tile_pool(name="const", bufs=1))
         gauss_pool = ctx.enter_context(tc.tile_pool(name="gauss", bufs=GROUP_BUFS))
         small = ctx.enter_context(tc.tile_pool(name="small", bufs=6))
-        grouped_pool = ctx.enter_context(tc.tile_pool(name="grouped", bufs=3))
+        grouped_pool = ctx.enter_context(tc.tile_pool(name="grouped", bufs=2))
         mx_pool = ctx.enter_context(tc.tile_pool(name="mx", bufs=4))
         pe_pool = ctx.enter_context(tc.tile_pool(name="pe", bufs=2))
         pe_mx_pool = ctx.enter_context(tc.tile_pool(name="pe_mx", bufs=4))
@@ -138,6 +138,30 @@ def tile_flashrecomodel_k_kernel(
             pattern=[[TICKS_LOW, TICKS // TICKS_LOW]],
             base=0,
             channel_multiplier=0,
+        )
+        flash_terms = const.tile([P, K_PASS], F32)
+        tick_terms = const.tile([P, TENSOR_COLS], F32)
+        stationaries = []
+        for copy in range(2):
+            stationary = const.tile([P, K_PASS], F32, name="stationary%d" % copy)
+            stationaries.append(stationary)
+        first_tick = TICKS - TENSOR_COLS
+        nc.gpsimd.iota(
+            out=tick_terms[64:128, :],
+            pattern=[[1, TENSOR_COLS]],
+            base=first_tick,
+            channel_multiplier=0,
+            allow_small_or_imprecise_dtypes=True,
+        )
+        nc.scalar.activation(
+            out=tick_terms[64:128, :], in_=tick_terms[64:128, :], func=ACT.Square
+        )
+        nc.gpsimd.iota(
+            out=tick_terms[0:32, :],
+            pattern=[[-2, TENSOR_COLS]],
+            base=-2 * first_tick,
+            channel_multiplier=0,
+            allow_small_or_imprecise_dtypes=True,
         )
         identity_bf = const.tile([P, P], BF16)
         make_identity(nc, identity_bf[:])
@@ -209,9 +233,9 @@ def tile_flashrecomodel_k_kernel(
                 gauss[g] = group_tile
             return gauss[g]
 
-        def differences_on_vector(g):
+        def differences_on_vector(g, which=slice(None)):
             if g < ALL_GROUPS:
-                for j, first, end in squares_of(g)[1]:
+                for j, first, end in squares_of(g)[1][which]:
                     nc.vector.tensor_scalar(
                         out=gauss_of(g)[:, j, first:end],
                         in0=ticks[:, first:end],
@@ -285,57 +309,6 @@ def tile_flashrecomodel_k_kernel(
                             scale=exp_scale[:, 0:1],
                             accum_out=first_sum[:, k : k + 1],
                         )
-
-        flash_terms = const.tile([P, K_PASS], F32)
-        tick_terms = const.tile([P, TENSOR_COLS], F32)
-        stationaries = []
-        for copy in range(2):
-            stationary = const.tile([P, K_PASS], F32, name="stationary%d" % copy)
-            stationaries.append(stationary)
-
-        def make_terms():
-            low = slice(0, ALL_GROUPS)
-            middle = slice(ALL_GROUPS, 2 * ALL_GROUPS)
-            high = slice(2 * ALL_GROUPS, P)
-            nc.vector.tensor_scalar(
-                out=flash_terms[0 : 2 * ALL_GROUPS, :],
-                in0=flash_rows[0 : 2 * ALL_GROUPS, :],
-                scalar1=float(TICKS),
-                scalar2=0.0,
-                op0=ALU.mult,
-                op1=ALU.max,
-            )
-            nc.vector.tensor_copy(out=tick_terms[low, :], in_=ticks[low, TICKS - TENSOR_COLS : TICKS])
-            nc.vector.tensor_scalar(
-                out=flash_terms[0 : 2 * ALL_GROUPS, :],
-                in0=flash_terms[0 : 2 * ALL_GROUPS, :],
-                scalar1=float(TICKS - 1),
-                scalar2=None,
-                op0=ALU.min,
-            )
-            nc.vector.tensor_tensor(
-                out=tick_terms[high, :],
-                in0=ticks[high, TICKS - TENSOR_COLS : TICKS],
-                in1=ticks[high, TICKS - TENSOR_COLS : TICKS],
-                op=ALU.mult,
-            )
-            nc.vector.tensor_scalar(
-                out=flash_terms[low, :],
-                in0=flash_terms[low, :],
-                scalar1=-2.0,
-                scalar2=None,
-                op0=ALU.mult,
-            )
-            nc.vector.tensor_tensor(
-                out=flash_terms[middle, :],
-                in0=flash_terms[middle, :],
-                in1=flash_terms[middle, :],
-                op=ALU.mult,
-            )
-            for stationary in stationaries:
-                nc.vector.memset(stationary[:], 0.0)
-            nc.vector.memset(tick_terms[middle, :], 1.0)
-            nc.vector.memset(flash_terms[high, :], 1.0)
 
         def squares_on_tensor(g):
             if g >= ALL_GROUPS or not tensor_planes(g):
@@ -431,18 +404,19 @@ def tile_flashrecomodel_k_kernel(
             pe_mx[g] = (codes, scales)
 
         w_grouped = {}
+        w_mx = {}
         acc = {}
 
-        def normalise(g, h):
-            grouped = grouped_pool.tile([P, HALF, PACK], BF16, align_bytes=64)
+        def normalise(g, end):
+            grouped = grouped_pool.tile([P, TICKS, PACK], BF16, align_bytes=64)
             factor = factors[g][:, 0:PACK].unsqueeze(1).unsqueeze(3)
             nc.vector.tensor_tensor(
-                out=words_view(grouped[:]),
-                in0=planes_view(gauss[g][:, :, h * HALF : (h + 1) * HALF]),
-                in1=factor.to_broadcast([P, HALF // RUN, PACK, RUN]),
+                out=words_view(grouped[:, 0:end, :]),
+                in0=planes_view(gauss[g][:, :, 0:end]),
+                in1=factor.to_broadcast([P, end // RUN, PACK, RUN]),
                 op=ALU.mult,
             )
-            w_grouped[(g, h)] = grouped
+            w_grouped[g] = grouped
 
         w_planes = const.tile([P, PACK, HALF], BF16)
 
@@ -456,19 +430,24 @@ def tile_flashrecomodel_k_kernel(
                 )
 
         def regroup(g, h):
-            grouped = grouped_pool.tile([P, HALF, PACK], BF16, align_bytes=64)
-            nc.vector.tensor_copy(out=words_view(grouped[:]), in_=planes_view(w_planes[:]))
-            w_grouped[(g, h)] = grouped
+            nc.vector.tensor_copy(
+                out=words_view(w_grouped[g][:, h * HALF : (h + 1) * HALF, :]),
+                in_=planes_view(w_planes[:]),
+            )
 
-        def quantise_and_multiply(g, h):
-            b, g_in_event = divmod(g, GROUPS)
+        def quantise(g, h):
             w_codes = mx_pool.tile([P, HALF], U32, align_bytes=64)
             w_scales = mx_pool.tile([P, HALF], U8, align_bytes=64)
             nc.vector.quantize_mx(
                 out=w_codes[:].bitcast(FP8X4),
                 scales=w_scales[:],
-                in_=w_grouped[(g, h)][:].rearrange("q t j -> q (t j)"),
+                in_=w_grouped[g][:, h * HALF : (h + 1) * HALF, :].rearrange("q t j -> q (t j)"),
             )
+            w_mx[(g, h)] = (w_codes, w_scales)
+
+        def multiply(g, h):
+            b, g_in_event = divmod(g, GROUPS)
+            w_codes, w_scales = w_mx[(g, h)]
             for n in range(BANKS_PER_HALF):
                 bank = h * BANKS_PER_HALF + n
                 if g_in_event == 0:
@@ -505,14 +484,41 @@ def tile_flashrecomodel_k_kernel(
             in_=by_flash[:, :, 2 * ALL_GROUPS : 3 * ALL_GROUPS],
         )
         differences_on_vector(1)
-        negated_centres(neg_centre[:].rearrange("q g j -> q j g"), by_flash[:, :, 0:ALL_GROUPS])
+        both = slice(0, 2 * ALL_GROUPS)
+        nc.vector.tensor_scalar(
+            out=flash_terms[both, :],
+            in0=flash_rows[both, :],
+            scalar1=float(TICKS),
+            scalar2=0.0,
+            op0=ALU.mult,
+            op1=ALU.max,
+        )
         squares_on_vector(1)
+        nc.vector.tensor_scalar(
+            out=flash_terms[both, :],
+            in0=flash_terms[both, :],
+            scalar1=float(TICKS - 1),
+            scalar2=None,
+            op0=ALU.min,
+        )
+        negated_centres(neg_centre[:].rearrange("q g j -> q j g"), by_flash[:, :, 0:ALL_GROUPS])
         gaussians_on_scalar(0)
         first_bank = factor_psum.tile([P, N_TILE], F32, name="bank")
         spread(first_bank, 0, confidence[:, 0, :])
         spread(first_bank, PACK, confidence[:, 1, :])
         for g in range(2):
             scale_pe(g, first_bank, g * PACK)
+        middle = slice(ALL_GROUPS, 2 * ALL_GROUPS)
+        nc.vector.tensor_tensor(
+            out=flash_terms[middle, :],
+            in0=flash_terms[middle, :],
+            in1=flash_terms[middle, :],
+            op=ALU.mult,
+        )
+        nc.vector.memset(tick_terms[32:64, :], 1.0)
+        nc.vector.memset(flash_terms[64:128, :], 1.0)
+        for stationary in stationaries:
+            nc.vector.memset(stationary[:], 0.0)
         for g in range(2):
             quantise_pe(g)
         add_eps(0)
@@ -524,26 +530,25 @@ def tile_flashrecomodel_k_kernel(
         spread_factors(0)
         for g in range(ALL_GROUPS):
             gaussians_on_scalar(g + 1)
-            normalise(g, 0)
+            normalise(g, TICKS if g < ALL_GROUPS - 1 else HALF)
             scale_pe(g + 2, factors[g], PACK)
             if g == GROUPS:
                 for bank in range(BANKS):
                     store_bank(0, bank, nc.vector.tensor_copy)
-            if g < ALL_GROUPS - 1:
-                normalise(g, 1)
-            else:
+            if g == ALL_GROUPS - 1:
                 normalise_on_scalar(g, 1)
                 regroup(g, 1)
-            quantise_and_multiply(g, 0)
+            quantise(g, 0)
+            multiply(g, 0)
             add_eps(g + 1)
             quantise_pe(g + 2)
+            differences_on_vector(g + 3, slice(0, 1))
             invert_sums(g + 1)
             spread_factors(g + 1)
-            if g == 0:
-                make_terms()
+            quantise(g, 1)
+            multiply(g, 1)
             squares_on_tensor(g + 2)
-            quantise_and_multiply(g, 1)
-            differences_on_vector(g + 3)
+            differences_on_vector(g + 3, slice(1, None))
             squares_on_gpsimd(g + 3)
             differences_on_gpsimd(g + 4)
         for bank in range(BANKS):

@@ -28,7 +28,7 @@ HALVES = 2
 HALF = TICKS // HALVES
 BANKS_PER_HALF = HALF // N_TILE
 PE_CHUNK = 4
-RUN = 4
+RUN = 8
 TICKS_LOW = 128
 EPS = 1e-10
 GPSIMD_COLS = 1280
@@ -51,7 +51,8 @@ def squares_of(g):
         return [], [(3, 0, TICKS), (1, 0, TICKS), (0, 0, HALF)], [(2, 0, TICKS), (0, HALF, TICKS)]
     if g == 1:
         return [], [(1, 0, TICKS)], [(2, 0, TICKS), (3, 0, TICKS), (0, 0, TICKS)]
-    quotas = [GPSIMD_COLS, SHARED_COLS - GPSIMD_COLS, PACK * TICKS]
+    gpsimd_cols = GPSIMD_COLS if g > 2 else 0
+    quotas = [gpsimd_cols, SHARED_COLS - gpsimd_cols, PACK * TICKS]
     pieces = [[], [], []]
     engine = 0
     for j in range(PACK):
@@ -91,8 +92,8 @@ def tile_flashrecomodel_k_kernel(
         pe_mx_pool = ctx.enter_context(tc.tile_pool(name="pe_mx", bufs=4))
         out_pool = ctx.enter_context(tc.tile_pool(name="result", bufs=4))
         psum = ctx.enter_context(tc.psum_pool(name="acc", bufs=1))
-        factor_psum = ctx.enter_context(tc.psum_pool(name="factor", bufs=1))
-        square_psum = ctx.enter_context(tc.psum_pool(name="square", bufs=3))
+        factor_psum = ctx.enter_context(tc.psum_pool(name="factor", bufs=2))
+        square_psum = ctx.enter_context(tc.psum_pool(name="square", bufs=2))
         ctx.enter_context(tc.manual_schedule())
 
         flash_rows = const.tile([P, K_PASS], BF16)
@@ -506,8 +507,11 @@ def tile_flashrecomodel_k_kernel(
         first_bank = factor_psum.tile([P, N_TILE], F32, name="bank")
         spread(first_bank, 0, confidence[:, 0, :])
         spread(first_bank, PACK, confidence[:, 1, :])
-        for g in range(2):
-            scale_pe(g, first_bank, g * PACK)
+        scale_pe(0, first_bank, 0)
+        add_eps(0)
+        scale_pe(1, first_bank, PACK)
+        invert_sums(0)
+        spread_factors(0)
         middle = slice(ALL_GROUPS, 2 * ALL_GROUPS)
         nc.vector.tensor_tensor(
             out=flash_terms[middle, :],
@@ -521,13 +525,9 @@ def tile_flashrecomodel_k_kernel(
             nc.vector.memset(stationary[:], 0.0)
         for g in range(2):
             quantise_pe(g)
-        add_eps(0)
         differences_on_vector(2)
-        differences_on_gpsimd(2)
         squares_on_gpsimd(2)
         differences_on_gpsimd(3)
-        invert_sums(0)
-        spread_factors(0)
         for g in range(ALL_GROUPS):
             gaussians_on_scalar(g + 1)
             normalise(g, TICKS if g < ALL_GROUPS - 1 else HALF)

from contextlib import ExitStack

import concourse.mybir as mybir
from concourse.masks import make_identity

F32 = mybir.dt.float32
BF16 = mybir.dt.bfloat16
I32 = mybir.dt.int32
U32 = mybir.dt.uint32
U8 = mybir.dt.uint8
FP8X4 = mybir.dt.float8_e4m3fn_x4
ALU = mybir.AluOpType
ACT = mybir.ActivationFunctionType

P = 128
PACK = 4
K_PASS = P * PACK
EVENTS = 2
FLASHES = 8192
CHANNELS = 128
TICKS = 2048
GROUPS = FLASHES // K_PASS
ALL_GROUPS = EVENTS * GROUPS
ALL_PLANES = ALL_GROUPS * PACK
N_TILE = 512
BANKS = TICKS // N_TILE
HALVES = 2
HALF = TICKS // HALVES
BANKS_PER_HALF = HALF // N_TILE
PE_CHUNK = 4
RUN = 8
TICKS_LOW = 128
EPS = 1e-10
GPSIMD_COLS = 1280
SHARED_COLS = 3456
TENSOR_COLS = 512
TENSOR_GROUPS = 25
EXP_ORDER = [2, 3, 1, 0]
GROUP_BUFS = 4
FIRST_GROUPS = 2

FLOPS = 2 * EVENTS * FLASHES * CHANNELS * TICKS


def tensor_planes(g):
    return [2, 3] if g >= ALL_GROUPS - TENSOR_GROUPS else []


def squares_of(g):
    if g == 0:
        return [], [(3, 0, TICKS), (1, 0, TICKS), (0, 0, HALF)], [(2, 0, TICKS), (0, HALF, TICKS)]
    if g == 1:
        return [], [(1, 0, TICKS)], [(2, 0, TICKS), (3, 0, TICKS), (0, 0, TICKS)]
    gpsimd_cols = GPSIMD_COLS if g > 2 else 0
    quotas = [gpsimd_cols, SHARED_COLS - gpsimd_cols, PACK * TICKS]
    pieces = [[], [], []]
    engine = 0
    for j in range(PACK):
        first = 0
        plane_end = TICKS - TENSOR_COLS if j in tensor_planes(g) else TICKS
        while first < plane_end:
            while quotas[engine] == 0:
                engine += 1
            end = min(plane_end, first + quotas[engine])
            pieces[engine].append((j, first, end))
            quotas[engine] -= end - first
            first = end
    return pieces


def planes_view(planes):
    return planes.rearrange("q j (c i) -> q c j i", i=RUN)


def words_view(grouped):
    return grouped.rearrange("q (c i) j -> q c j i", i=RUN)


def tile_flashrecomodel_k_kernel(
    tc, flashes_pe, flashes_time, flashes_confidence, num_ticks, sigma, out
):
    nc = tc.nc
    assert num_ticks == TICKS

    with ExitStack() as ctx:
        const = ctx.enter_context(tc.tile_pool(name="const", bufs=1))
        gauss_pool = ctx.enter_context(tc.tile_pool(name="gauss", bufs=GROUP_BUFS))
        small = ctx.enter_context(tc.tile_pool(name="small", bufs=6))
        grouped_pool = ctx.enter_context(tc.tile_pool(name="grouped", bufs=2))
        mx_pool = ctx.enter_context(tc.tile_pool(name="mx", bufs=4))
        pe_pool = ctx.enter_context(tc.tile_pool(name="pe", bufs=2))
        pe_mx_pool = ctx.enter_context(tc.tile_pool(name="pe_mx", bufs=4))
        out_pool = ctx.enter_context(tc.tile_pool(name="result", bufs=4))
        psum = ctx.enter_context(tc.psum_pool(name="acc", bufs=1))
        factor_psum = ctx.enter_context(tc.psum_pool(name="factor", bufs=2))
        square_psum = ctx.enter_context(tc.psum_pool(name="square", bufs=2))
        ctx.enter_context(tc.manual_schedule())

        flash_rows = const.tile([P, K_PASS], BF16)
        nc.vector.memset(flash_rows[:], 0.0)
        first_times = const.tile([P, FIRST_GROUPS, PACK], BF16)
        nc.sync.dma_start(
            out=first_times[:],
            in_=flashes_time[0, 0 : FIRST_GROUPS * K_PASS, :].rearrange(
                "(g q j) o -> q g (j o)", q=P, j=PACK
            ),
        )
        for copy in range(2):
            nc.sync.dma_start(
                out=flash_rows[copy * ALL_GROUPS : (copy + 1) * ALL_GROUPS, :],
                in_=flashes_time.rearrange("b (g k) o -> (b g) (k o)", k=K_PASS),
            )
        nc.scalar.dma_start(
            out=flash_rows[2 * ALL_GROUPS : 3 * ALL_GROUPS, :],
            in_=flashes_confidence.rearrange("b (g k) o -> (b g) (k o)", k=K_PASS),
        )
        sigma_bf = const.tile([P, 1], BF16)
        nc.scalar.dma_start(out=sigma_bf[:], in_=sigma.partition_broadcast(P))
        pe_raw = {}

        def load_pe(chunk):
            b, first = divmod(chunk * PE_CHUNK, GROUPS)
            raw = pe_pool.tile([P, PE_CHUNK, PACK, CHANNELS], BF16)
            nc.sync.dma_start(
                out=raw[:].rearrange("q g j c -> q g (j c)"),
                in_=flashes_pe[b].rearrange("(g q j) c -> q g (j c)", q=P, j=PACK)[
                    :, first : first + PE_CHUNK, :
                ],
            )
            pe_raw[chunk] = raw

        load_pe(0)

        tick_low = const.tile([P, TICKS_LOW], I32)
        nc.gpsimd.iota(out=tick_low[:], pattern=[[1, TICKS_LOW]], base=0, channel_multiplier=0)
        tick_high = const.tile([P, TICKS // TICKS_LOW], I32)
        nc.gpsimd.iota(
            out=tick_high[:],
            pattern=[[TICKS_LOW, TICKS // TICKS_LOW]],
            base=0,
            channel_multiplier=0,
        )
        flash_terms = const.tile([P, K_PASS], F32)
        tick_terms = const.tile([P, TENSOR_COLS], F32)
        stationaries = []
        for copy in range(2):
            stationary = const.tile([P, K_PASS], F32, name="stationary%d" % copy)
            stationaries.append(stationary)
        first_tick = TICKS - TENSOR_COLS
        nc.gpsimd.iota(
            out=tick_terms[64:128, :],
            pattern=[[1, TENSOR_COLS]],
            base=first_tick,
            channel_multiplier=0,
            allow_small_or_imprecise_dtypes=True,
        )
        nc.scalar.activation(
            out=tick_terms[64:128, :], in_=tick_terms[64:128, :], func=ACT.Square
        )
        nc.gpsimd.iota(
            out=tick_terms[0:32, :],
            pattern=[[-2, TENSOR_COLS]],
            base=-2 * first_tick,
            channel_multiplier=0,
            allow_small_or_imprecise_dtypes=True,
        )
        identity_bf = const.tile([P, P], BF16)
        make_identity(nc, identity_bf[:])
        identity = const.tile([P, P], F32)
        make_identity(nc, identity[:])
        ticks = const.tile([P, TICKS], F32)
        high_low = [P, TICKS // TICKS_LOW, TICKS_LOW]
        nc.vector.tensor_tensor(
            out=ticks[:].rearrange("q (h l) -> q h l", l=TICKS_LOW),
            in0=tick_high[:].unsqueeze(2).to_broadcast(high_low),
            in1=tick_low[:].unsqueeze(1).to_broadcast(high_low),
            op=ALU.add,
        )

        by_flash = square_psum.tile([P, PACK, P], BF16, name="square")
        for j in range(PACK):
            nc.tensor.transpose(by_flash[:, j, :], flash_rows[:, j::PACK], identity_bf[:])

        def negated_centres(out, times):
            nc.vector.tensor_scalar(
                out=out,
                in0=times,
                scalar1=float(TICKS),
                scalar2=0.0,
                op0=ALU.mult,
                op1=ALU.max,
            )
            nc.vector.tensor_scalar(
                out=out,
                in0=out,
                scalar1=float(TICKS - 1),
                scalar2=-1.0,
                op0=ALU.min,
                op1=ALU.mult,
            )

        first_centre = const.tile([P, FIRST_GROUPS, PACK], F32)
        negated_centres(first_centre[:], first_times[:])
        neg_centre = const.tile([P, ALL_GROUPS, PACK], F32)

        def centre(g, j):
            return (first_centre if g < FIRST_GROUPS else neg_centre)[:, g, j : j + 1]

        neg_two_var = const.tile([P, 1], F32)
        nc.vector.scalar_tensor_tensor(
            out=neg_two_var[:],
            in0=sigma_bf[:],
            scalar=-2.0,
            in1=sigma_bf[:],
            op0=ALU.mult,
            op1=ALU.mult,
        )
        exp_scale = const.tile([P, 1], F32)
        nc.vector.reciprocal(out=exp_scale[:], in_=neg_two_var[:])

        gauss = {}
        spare_sums = []
        for copy in range(2):
            spare_sum = const.tile([P, PACK], F32, name="spare_sum%d" % copy)
            nc.gpsimd.memset(spare_sum[:], 0.0)
            spare_sums.append(spare_sum)
        tick_sums = {}
        first_sums = {}
        tensor_squares = {}

        def gauss_of(g):
            if g not in gauss:
                group_tile = gauss_pool.tile([P, PACK, TICKS], F32)
                gauss[g] = group_tile
            return gauss[g]

        def differences_on_vector(g, which=slice(None)):
            if g < ALL_GROUPS:
                for j, first, end in squares_of(g)[1][which]:
                    nc.vector.tensor_scalar(
                        out=gauss_of(g)[:, j, first:end],
                        in0=ticks[:, first:end],
                        scalar1=centre(g, j),
                        scalar2=None,
                        op0=ALU.add,
                    )

        def squares_on_vector(g):
            if g < ALL_GROUPS:
                for j, first, end in squares_of(g)[1]:
                    piece = gauss_of(g)[:, j, first:end]
                    nc.vector.tensor_tensor(out=piece, in0=piece, in1=piece, op=ALU.mult)

        def differences_on_gpsimd(g):
            if g >= ALL_GROUPS:
                return
            for j, first, end in squares_of(g)[0]:
                nc.gpsimd.tensor_scalar(
                    out=gauss_of(g)[:, j, first:end],
                    in0=ticks[:, first:end],
                    scalar1=centre(g, j),
                    scalar2=1.0,
                    op0=ALU.add,
                    op1=ALU.mult,
                )

        def squares_on_gpsimd(g):
            if g >= ALL_GROUPS:
                return
            piece = gauss_of(g)[:].rearrange("q j t -> q (j t)")[:, 0:SHARED_COLS]
            nc.gpsimd.tensor_tensor(out=piece, in0=piece, in1=piece, op=ALU.mult)

        def square_on_scalar(g, piece):
            j, first, end = piece
            nc.scalar.activation(
                out=gauss_of(g)[:, j, first:end],
                in_=ticks[:, first:end],
                func=ACT.Square,
                bias=centre(g, j),
                scale=1.0,
            )

        def gaussians_on_scalar(g):
            if g >= ALL_GROUPS:
                return
            for piece in squares_of(g)[2][: 1 if g == 0 else None]:
                square_on_scalar(g, piece)
            tick_sum = small.tile([P, PACK], F32)
            tick_sums[g] = tick_sum
            for j in EXP_ORDER:
                end = TICKS - TENSOR_COLS if j in tensor_planes(g) else TICKS
                piece = gauss_of(g)[:, j, 0:end]
                nc.scalar.activation(
                    out=piece,
                    in_=piece,
                    func=ACT.Exp,
                    scale=exp_scale[:, 0:1],
                    accum_out=tick_sum[:, j : j + 1],
                )
                if g == 0 and j == 2:
                    square_on_scalar(0, squares_of(0)[2][1])
                if j == EXP_ORDER[1] and tensor_planes(g):
                    first_sum = spare_sums[g % 2]
                    first_sums[g] = first_sum
                    for k in tensor_planes(g):
                        nc.scalar.activation(
                            out=gauss_of(g)[:, k, TICKS - TENSOR_COLS : TICKS],
                            in_=tensor_squares[(g, k)][:],
                            func=ACT.Exp,
                            scale=exp_scale[:, 0:1],
                            accum_out=first_sum[:, k : k + 1],
                        )

        def squares_on_tensor(g):
            if g >= ALL_GROUPS or not tensor_planes(g):
                return
            stationary = stationaries[g % 2]
            nc.sync.dma_start(
                out=stationary[0 : 2 * ALL_GROUPS + 1 : ALL_GROUPS, :],
                in_=flash_terms[g : g + 2 * ALL_GROUPS + 1 : ALL_GROUPS, :],
            )
            for j in tensor_planes(g):
                square = square_psum.tile([P, TENSOR_COLS], F32)
                nc.tensor.matmul(
                    out=square[:],
                    lhsT=stationary[:, j::PACK],
                    rhs=tick_terms[:],
                    start=True,
                    stop=True,
                )
                tensor_squares[(g, j)] = square

        confidence = const.tile([P, ALL_GROUPS, PACK], F32)
        inv_sums = {}
        factors = {}

        def add_eps(g):
            if g < ALL_GROUPS:
                inv_sum = small.tile([P, PACK], F32)
                if g in first_sums:
                    nc.vector.scalar_tensor_tensor(
                        out=inv_sum[:],
                        in0=tick_sums[g][:],
                        scalar=EPS,
                        in1=first_sums[g][:],
                        op0=ALU.add,
                        op1=ALU.add,
                    )
                else:
                    nc.vector.tensor_scalar(
                        out=inv_sum[:], in0=tick_sums[g][:], scalar1=EPS, scalar2=None, op0=ALU.add
                    )
                inv_sums[g] = inv_sum

        def invert_sums(g):
            if g < ALL_GROUPS:
                nc.vector.reciprocal(out=inv_sums[g][:], in_=inv_sums[g][:])

        def spread(bank, first, values):
            nc.tensor.matmul(
                out=bank[:, first : first + PACK],
                lhsT=identity[:],
                rhs=values,
                start=True,
                stop=True,
            )

        def spread_factors(g):
            if g < ALL_GROUPS:
                bank = factor_psum.tile([P, N_TILE], F32)
                spread(bank, 0, inv_sums[g][:])
                if g + 2 < ALL_GROUPS:
                    spread(bank, PACK, confidence[:, g + 2, :])
                factors[g] = bank

        pe_grouped = {}
        pe_mx = {}

        def scale_pe(g, bank, first):
            if g >= ALL_GROUPS:
                return
            chunk, k = divmod(g, PE_CHUNK)
            if k == 0 and chunk + 1 < ALL_GROUPS // PE_CHUNK:
                load_pe(chunk + 1)
            grouped = pe_mx_pool.tile([P, CHANNELS, PACK], BF16, align_bytes=64, name="pe_grouped")
            factor = bank[:, first : first + PACK].unsqueeze(1).unsqueeze(3)
            nc.vector.tensor_tensor(
                out=words_view(grouped[:]),
                in0=planes_view(pe_raw[chunk][:, k, :, :]),
                in1=factor.to_broadcast([P, CHANNELS // RUN, PACK, RUN]),
                op=ALU.mult,
            )
            pe_grouped[g] = grouped

        def quantise_pe(g):
            if g >= ALL_GROUPS:
                return
            codes = pe_mx_pool.tile([P, CHANNELS], U32, align_bytes=64, name="pe_codes")
            scales = pe_mx_pool.tile([P, CHANNELS], U8, align_bytes=64, name="pe_scales")
            nc.vector.quantize_mx(
                out=codes[:].bitcast(FP8X4),
                scales=scales[:],
                in_=pe_grouped[g][:].rearrange("q c j -> q (c j)"),
            )
            pe_mx[g] = (codes, scales)

        w_grouped = {}
        w_mx = {}
        acc = {}

        def normalise(g, end):
            grouped = grouped_pool.tile([P, TICKS, PACK], BF16, align_bytes=64)
            factor = factors[g][:, 0:PACK].unsqueeze(1).unsqueeze(3)
            nc.vector.tensor_tensor(
                out=words_view(grouped[:, 0:end, :]),
                in0=planes_view(gauss[g][:, :, 0:end]),
                in1=factor.to_broadcast([P, end // RUN, PACK, RUN]),
                op=ALU.mult,
            )
            w_grouped[g] = grouped

        w_planes = const.tile([P, PACK, HALF], BF16)

        def normalise_on_scalar(g, h):
            for j in range(PACK):
                nc.scalar.activation(
                    out=w_planes[:, j, :],
                    in_=gauss[g][:, j, h * HALF : (h + 1) * HALF],
                    func=ACT.Copy,
                    scale=inv_sums[g][:, j : j + 1],
                )

        def regroup(g, h):
            nc.vector.tensor_copy(
                out=words_view(w_grouped[g][:, h * HALF : (h + 1) * HALF, :]),
                in_=planes_view(w_planes[:]),
            )

        def quantise(g, h):
            w_codes = mx_pool.tile([P, HALF], U32, align_bytes=64)
            w_scales = mx_pool.tile([P, HALF], U8, align_bytes=64)
            nc.vector.quantize_mx(
                out=w_codes[:].bitcast(FP8X4),
                scales=w_scales[:],
                in_=w_grouped[g][:, h * HALF : (h + 1) * HALF, :].rearrange("q t j -> q (t j)"),
            )
            w_mx[(g, h)] = (w_codes, w_scales)

        def multiply(g, h):
            b, g_in_event = divmod(g, GROUPS)
            w_codes, w_scales = w_mx[(g, h)]
            for n in range(BANKS_PER_HALF):
                bank = h * BANKS_PER_HALF + n
                if g_in_event == 0:
                    acc[(b, bank)] = psum.tile([CHANNELS, N_TILE], F32, name="acc%d" % bank)
                cols = slice(n * N_TILE, (n + 1) * N_TILE)
                nc.tensor.matmul_mx(
                    out=acc[(b, bank)][:],
                    lhsT=pe_mx[g][0][:].bitcast(FP8X4),
                    lhsT_scale=pe_mx[g][1][:],
                    rhs=w_codes[:, cols].bitcast(FP8X4),
                    rhs_scale=w_scales[:, cols],
                    start=(g_in_event == 0),
                    stop=(g_in_event == GROUPS - 1),
                )

        def store_bank(b, bank, copy):
            result = out_pool.tile([CHANNELS, N_TILE], F32)
            copy(out=result[:], in_=acc[(b, bank)][:])
            nc.sync.dma_start(out=out[b, :, bank * N_TILE : (bank + 1) * N_TILE], in_=result[:])

        for piece in range(len(squares_of(0)[1])):
            j, first, end = squares_of(0)[1][piece]
            plane = gauss_of(0)[:, j, first:end]
            nc.vector.tensor_scalar(
                out=plane,
                in0=ticks[:, first:end],
                scalar1=centre(0, j),
                scalar2=None,
                op0=ALU.add,
            )
            nc.vector.tensor_tensor(out=plane, in0=plane, in1=plane, op=ALU.mult)
        nc.vector.tensor_copy(
            out=confidence[:].rearrange("q g j -> q j g"),
            in_=by_flash[:, :, 2 * ALL_GROUPS : 3 * ALL_GROUPS],
        )
        differences_on_vector(1)
        both = slice(0, 2 * ALL_GROUPS)
        nc.vector.tensor_scalar(
            out=flash_terms[both, :],
            in0=flash_rows[both, :],
            scalar1=float(TICKS),
            scalar2=0.0,
            op0=ALU.mult,
            op1=ALU.max,
        )
        squares_on_vector(1)
        nc.vector.tensor_scalar(
            out=flash_terms[both, :],
            in0=flash_terms[both, :],
            scalar1=float(TICKS - 1),
            scalar2=None,
            op0=ALU.min,
        )
        negated_centres(neg_centre[:].rearrange("q g j -> q j g"), by_flash[:, :, 0:ALL_GROUPS])
        gaussians_on_scalar(0)
        first_bank = factor_psum.tile([P, N_TILE], F32, name="bank")
        spread(first_bank, 0, confidence[:, 0, :])
        spread(first_bank, PACK, confidence[:, 1, :])
        scale_pe(0, first_bank, 0)
        add_eps(0)
        scale_pe(1, first_bank, PACK)
        invert_sums(0)
        spread_factors(0)
        middle = slice(ALL_GROUPS, 2 * ALL_GROUPS)
        nc.vector.tensor_tensor(
            out=flash_terms[middle, :],
            in0=flash_terms[middle, :],
            in1=flash_terms[middle, :],
            op=ALU.mult,
        )
        nc.vector.memset(tick_terms[32:64, :], 1.0)
        nc.vector.memset(flash_terms[64:128, :], 1.0)
        for stationary in stationaries:
            nc.vector.memset(stationary[:], 0.0)
        for g in range(2):
            quantise_pe(g)
        differences_on_vector(2)
        squares_on_gpsimd(2)
        differences_on_gpsimd(3)
        for g in range(ALL_GROUPS):
            gaussians_on_scalar(g + 1)
            normalise(g, TICKS if g < ALL_GROUPS - 1 else HALF)
            scale_pe(g + 2, factors[g], PACK)
            if g == GROUPS:
                for bank in range(BANKS):
                    store_bank(0, bank, nc.vector.tensor_copy)
            if g == ALL_GROUPS - 1:
                normalise_on_scalar(g, 1)
                regroup(g, 1)
            quantise(g, 0)
            multiply(g, 0)
            add_eps(g + 1)
            quantise_pe(g + 2)
            differences_on_vector(g + 3, slice(0, 1))
            invert_sums(g + 1)
            spread_factors(g + 1)
            quantise(g, 1)
            multiply(g, 1)
            squares_on_tensor(g + 2)
            differences_on_vector(g + 3, slice(1, None))
            squares_on_gpsimd(g + 3)
            differences_on_gpsimd(g + 4)
        for bank in range(BANKS):
            store_bank(1, bank, nc.vector.tensor_copy if bank % 2 else nc.scalar.copy)
